import numpy as np
import ml_dtypes


def mxq(x, axis, fmt="e4m3"):
    dtype, down = {"e4m3": (ml_dtypes.float8_e4m3fn, 7), "e5m2": (ml_dtypes.float8_e5m2, 14)}[fmt]
    v = np.moveaxis(np.asarray(x, np.float32).astype(ml_dtypes.bfloat16).astype(np.float64), axis, -1)
    blocks = v.reshape(v.shape[:-1] + (-1, 32))
    amax = np.abs(blocks).max(-1, keepdims=True)
    byte = np.maximum(np.where(amax > 0, np.frexp(amax)[1] - 1 + 127, 0) - down, 1)
    scale = np.exp2(byte - 127.0)
    codes = (blocks / scale).astype(np.float32).astype(dtype).astype(np.float64)
    return np.moveaxis((codes * scale).reshape(v.shape), -1, axis)


WIDE = False


def mx_kscale(k):
    if not WIDE:
        return np.ones(k)
    levels = np.array([10, -10, 5, -5, 0])
    a = np.random.permutation(np.resize(levels, k // 512 * 4)).reshape(k // 512, 4)
    idx = np.arange(k)
    return np.exp2(a[idx // 512, idx % 128 // 32])


BF16 = ml_dtypes.bfloat16


def bf(x):
    return np.asarray(x, np.float32).astype(BF16)


def f64(x):
    return np.asarray(x).astype(np.float64)


E2M1 = np.array([0.0, 0.5, 1.0, 1.5, 2.0, 3.0, 4.0, 6.0, -0.0, -0.5, -1.0, -1.5, -2.0, -3.0, -4.0, -6.0])


def pack_weight(w, fmt):
    k, n = w.shape
    w = f64(bf(w)).reshape(k // 32, 32, n)
    amax = np.abs(w).max(1)
    if fmt == "e4m3":
        byte = np.frexp(amax)[1] - 1 + 127 - 7
    else:
        mant, ex = np.frexp(amax / 6.0)
        byte = np.where(mant > 0.5, ex, ex - 1) + 127
    byte = np.clip(np.where(amax > 0, byte, 1), 1, 254)
    scaled = (w * np.exp2(127.0 - byte)[:, None, :]).reshape(k, n).astype(np.float32)
    by_word = np.ascontiguousarray(scaled.reshape(k // 512, 128, 4, n).transpose(0, 1, 3, 2))
    if fmt == "e4m3":
        words = by_word.astype(ml_dtypes.float8_e4m3fn).view(np.uint8)
    else:
        c = by_word.astype(ml_dtypes.float4_e2m1fn).view(np.uint8) & 0xF
        words = c[..., 0::2] | (c[..., 1::2] << 4)
    return np.ascontiguousarray(words), np.ascontiguousarray(byte.astype(np.uint8).reshape(k // 512, 16, n))


def unpack_weight(words, scales, fmt):
    g, p, n, _ = words.shape
    if fmt == "e4m3":
        vals = np.ascontiguousarray(words).view(ml_dtypes.float8_e4m3fn).astype(np.float64)
    else:
        nib = np.empty((g, p, n, 4), np.uint8)
        nib[..., 0::2] = words & 0xF
        nib[..., 1::2] = words >> 4
        vals = E2M1[nib]
    vals = vals * np.repeat(np.exp2(scales.astype(np.float64) - 127.0), 8, axis=1)[..., None]
    return vals.transpose(0, 1, 3, 2).reshape(g * 512, n)

def pack4(w):
    words, scales = pack_weight(w, "e2m1")
    return words.reshape(words.shape[0], 128, -1), scales


def unpack4(words, scales):
    return unpack_weight(words.reshape(words.shape[0], 128, -1, 2), scales, "e2m1")


B, C, H, W = 2, 1024, 32, 32
C2 = C + C


def setup_inputs():
    s = mx_kscale(C)
    x = bf(np.random.standard_normal((B, C, H, W)) * s[None, :, None, None])
    mask = bf(np.random.random_sample((B, 1, H, W)))
    words, scales = pack4(np.random.standard_normal((C, C2)) / np.sqrt(C) / s[:, None])
    b_kv = bf(np.random.standard_normal(C2) * 0.3)
    return {"x": x,
            "mask": mask,
            "W_kv_words": words,
            "W_kv_scales": scales,
            "b_kv": b_kv}


def reference(x, mask, W_kv_words, W_kv_scales, b_kv):
    x, mask = f64(x), f64(mask)
    b, c, h, w = x.shape
    xf = np.transpose(x, (0, 2, 3, 1)).reshape(b, h * w, c)
    kv = (mxq(xf, 2, "e4m3") @ unpack4(W_kv_words, W_kv_scales)) + f64(b_kv)
    k, v = kv[..., :c], kv[..., c:]
    k = k / np.linalg.norm(k, axis=-1, keepdims=True)
    m = np.transpose(mask, (0, 2, 3, 1)).reshape(b, h * w, 1)
    inv = 1.0 - m
    ku = k * inv
    km = k * m
    kv_know = np.sum(ku * v, axis=-2, keepdims=True)
    kv_mask = np.sum(km * v, axis=-2, keepdims=True)
    return kv_know, kv_mask

@@ -1,0 +1,219 @@
+from contextlib import ExitStack
+
+import concourse.mybir as mybir
+from concourse.masks import make_identity
+
+F32 = mybir.dt.float32
+BF16 = mybir.dt.bfloat16
+U8 = mybir.dt.uint8
+U32 = mybir.dt.uint32
+I32 = mybir.dt.int32
+FP8X4 = mybir.dt.float8_e4m3fn_x4
+FP4X4 = mybir.dt.float4_e2m1fn_x4
+ADD = mybir.AluOpType.add
+MULT = mybir.AluOpType.mult
+ACT = mybir.ActivationFunctionType
+
+IMAGES = 2
+CHANNELS = 1024
+PIXELS = 1024
+KV = 2 * CHANNELS
+
+P = 128
+PACK = 4
+K_PASS = P * PACK
+PASSES = CHANNELS // K_PASS
+BANK = 512
+BANKS_PER_TILE = KV // BANK
+KEY_BANKS = CHANNELS // BANK
+TILES_PER_IMAGE = PIXELS // P
+TILES = IMAGES * TILES_PER_IMAGE
+CHUNK_TILES = 2
+CHUNK = CHUNK_TILES * P
+CHUNKS = TILES // CHUNK_TILES
+CHUNKS_PER_IMAGE = PIXELS // CHUNK
+BLOCKS = CHANNELS // P
+SUMS = 2
+ROWS = IMAGES * BLOCKS
+
+FLOPS = 2 * IMAGES * PIXELS * CHANNELS * KV
+
+
+def tile_hydraattention_pa_kernel(tc, x, mask, W_kv_words, W_kv_scales, b_kv, out_0, out_1):
+    nc = tc.nc
+    with ExitStack() as ctx:
+        keep = ctx.enter_context(tc.tile_pool(name="keep", bufs=1))
+        stage = ctx.enter_context(tc.tile_pool(name="stage", bufs=2))
+        work = ctx.enter_context(tc.tile_pool(name="work", bufs=3))
+        prods = ctx.enter_context(tc.tile_pool(name="prods", bufs=4))
+        psum = ctx.enter_context(tc.psum_pool(name="psum", bufs=7))
+        psum_sums = ctx.enter_context(tc.psum_pool(name="psum_sums", bufs=1))
+        ctx.enter_context(tc.manual_schedule())
+
+        raw = keep.tile([P, CHUNKS, PACK, PASSES * CHUNK], BF16)
+        x_codes = keep.tile([P, CHUNKS, PASSES * CHUNK], U32, align_bytes=64)
+        x_scales = keep.tile([P, CHUNKS, PASSES * CHUNK], U8, align_bytes=64)
+        w_words = keep.tile([P, PASSES, 2 * KV], U8, align_bytes=64)
+        w_planes = keep.tile([P, PASSES, KV], U8, align_bytes=64)
+        bias = keep.tile([P, KV], BF16)
+        ident = keep.tile([P, P], F32)
+        mask_rows = keep.tile([P, P], BF16)
+        mask_f32 = keep.tile([P, P], F32)
+        mask_pair = keep.tile([P, TILES, SUMS], F32)
+        sumsq = keep.tile([P, TILES], F32)
+        norm = keep.tile([P, TILES], F32)
+        inv_norm = keep.tile([P, TILES], F32)
+        weights = keep.tile([P, TILES, SUMS], F32)
+        sums = keep.tile([P, P], F32)
+        rows = keep.tile([P, P], F32)
+        one = keep.tile([P, 1], F32)
+        one_root = keep.tile([P, 1], F32)
+        pooled = psum_sums.tile([P, TILES, BLOCKS, SUMS], F32)
+
+        nc.vector.memset(w_planes[:].rearrange("p g n -> p (g n)").bitcast(I32), 0)
+        nc.vector.memset(one[:], 1.0)
+        nc.scalar.sqrt(out=one_root[:], in_=one[:])
+        nc.gpsimd.memset(mask_rows[:], 0.0)
+        nc.gpsimd.memset(sums[:], 0.0)
+        make_identity(nc, ident[:])
+
+        x_rows = x.rearrange("b (g p j) h w -> b g p j (h w)", g=PASSES, p=P, j=PACK)
+
+        def load_chunk(c):
+            b, part = divmod(c, CHUNKS_PER_IMAGE)
+            for g in range(PASSES):
+                nc.sync.dma_start(
+                    out=raw[:, c, :, g * CHUNK : (g + 1) * CHUNK],
+                    in_=x_rows[b, g, :, :, part * CHUNK : (part + 1) * CHUNK],
+                )
+
+        def load_words(first_byte, last_byte):
+            nc.sync.dma_start(
+                out=w_words[:, :, first_byte:last_byte].bitcast(I32),
+                in_=W_kv_words.rearrange("g p n -> p g n")[:, :, first_byte:last_byte].bitcast(I32),
+            )
+
+        load_chunk(0)
+        load_words(0, KV)
+        for r in range(PACK):
+            nc.sync.dma_start(
+                out=w_planes[r:P:32, :, :].bitcast(I32),
+                in_=W_kv_scales[:, r : 4 * PACK : PACK, :].rearrange("g q n -> q g n").bitcast(I32),
+            )
+        nc.sync.dma_start(out=bias[:], in_=b_kv.partition_broadcast(P))
+        load_words(KV, 2 * KV)
+        load_chunk(1)
+        nc.sync.dma_start(
+            out=mask_rows[0:TILES, :],
+            in_=mask.rearrange("b o (i r) w -> (b o i) (r w)", i=TILES_PER_IMAGE),
+        )
+        for c in range(2, CHUNKS):
+            load_chunk(c)
+
+        def regroup(copy, c):
+            grouped = stage.tile([P, PASSES * CHUNK, PACK], BF16, align_bytes=64)
+            copy(
+                out=grouped[:].rearrange("p (c i) j -> p c j i", i=4),
+                in_=raw[:, c].rearrange("p j (c i) -> p c j i", i=4),
+            )
+            return grouped
+
+        def quantise(c, grouped):
+            nc.vector.quantize_mx(
+                out=x_codes[:, c, :].bitcast(FP8X4),
+                scales=x_scales[:, c, :],
+                in_=grouped[:].rearrange("p w j -> p (w j)"),
+            )
+
+        def project(t):
+            c, part = divmod(t, CHUNK_TILES)
+            banks = []
+            for n in range(BANKS_PER_TILE):
+                acc = psum.tile([P, BANK], F32, tag="acc")
+                for g in range(PASSES):
+                    px = slice(g * CHUNK + part * P, g * CHUNK + (part + 1) * P)
+                    nc.tensor.matmul_mx(
+                        out=acc[:],
+                        lhsT=x_codes[:, c, px].bitcast(FP8X4),
+                        lhsT_scale=x_scales[:, c, px],
+                        rhs=w_words[:, g, 2 * n * BANK : 2 * (n + 1) * BANK].bitcast(FP4X4),
+                        rhs_scale=w_planes[:, g, n * BANK : (n + 1) * BANK],
+                        start=(g == 0),
+                        stop=(g == PASSES - 1),
+                    )
+                banks.append(acc)
+            return banks
+
+        def multiply(t, banks):
+            kb = work.tile([P, CHANNELS], F32)
+            vb = work.tile([P, CHANNELS], F32)
+            squares = work.tile([P, CHANNELS], F32)
+            prod = prods.tile([P, CHANNELS], F32)
+            for n in range(BANKS_PER_TILE):
+                dst = kb if n < KEY_BANKS else vb
+                cols = slice((n % KEY_BANKS) * BANK, (n % KEY_BANKS + 1) * BANK)
+                nc.vector.tensor_tensor(
+                    out=dst[:, cols], in0=banks[n][:], in1=bias[:, n * BANK : (n + 1) * BANK], op=ADD
+                )
+            nc.scalar.activation(out=squares[:], in_=kb[:], func=ACT.Square, accum_out=sumsq[:, t : t + 1])
+            nc.gpsimd.tensor_tensor(out=prod[:], in0=kb[:], in1=vb[:], op=MULT)
+            return prod
+
+        def weigh(t):
+            nc.scalar.sqrt(out=norm[:, t : t + 1], in_=sumsq[:, t : t + 1])
+            nc.vector.reciprocal(out=inv_norm[:, t : t + 1], in_=norm[:, t : t + 1])
+            nc.vector.tensor_scalar(
+                out=weights[:, t, :], in0=mask_pair[:, t, :], scalar1=inv_norm[:, t : t + 1], scalar2=None, op0=MULT
+            )
+
+        def pool_pixels(t, prod):
+            for j in range(BLOCKS):
+                nc.tensor.matmul(
+                    out=pooled[:, t, j, :],
+                    lhsT=prod[:, j * P : (j + 1) * P],
+                    rhs=weights[:, t, :],
+                    start=True,
+                    stop=True,
+                )
+
+        grouped_of = {}
+        quantise(0, regroup(nc.vector.tensor_copy, 0))
+        grouped_of[1] = regroup(nc.scalar.copy, 1)
+        banks = project(0)
+
+        nc.scalar.copy(out=mask_f32[:], in_=mask_rows[:])
+        mask_cols = psum.tile([P, BANK], F32, tag="acc")
+        nc.tensor.transpose(out=mask_cols[:, 0:P], in_=mask_f32[:], identity=ident[:])
+        nc.scalar.activation(out=mask_pair[:, :, 0], in_=mask_cols[:, 0:TILES], func=ACT.Copy, scale=-1.0, bias=1.0)
+        nc.scalar.copy(out=mask_pair[:, :, 1], in_=mask_cols[:, 0:TILES])
+
+        prod_of = {}
+        for t in range(TILES + 1):
+            if t + 1 < TILES:
+                upcoming = project(t + 1)
+            if t < TILES:
+                prod_of[t] = multiply(t, banks)
+                banks = upcoming
+            if t >= 1:
+                weigh(t - 1)
+                pool_pixels(t - 1, prod_of[t - 1])
+            if (t + 3) % CHUNK_TILES == 0 and t + 3 < TILES:
+                grouped_of[(t + 3) // CHUNK_TILES] = regroup(nc.scalar.copy, (t + 3) // CHUNK_TILES)
+            if (t + 2) % CHUNK_TILES == 0 and t + 2 < TILES:
+                quantise((t + 2) // CHUNK_TILES, grouped_of[(t + 2) // CHUNK_TILES])
+
+        by_sum = pooled[:].rearrange("p (b i) j s -> p s b j i", b=IMAGES)
+        for s in range(SUMS):
+            nc.vector.tensor_reduce(
+                out=sums[:, s * ROWS : (s + 1) * ROWS].rearrange("p (b j) -> p b j", b=IMAGES),
+                in_=by_sum[:, s],
+                axis=mybir.AxisListType.X,
+                op=ADD,
+            )
+        turned = psum.tile([P, BANK], F32, tag="acc")
+        nc.tensor.transpose(out=turned[:, 0:P], in_=sums[:], identity=ident[:])
+        nc.vector.tensor_copy(out=rows[:], in_=turned[:, 0:P])
+        for s, out in enumerate((out_0, out_1)):
+            nc.sync.dma_start(
+                out=out.rearrange("b o (j n) -> (b o j) n", n=P), in_=rows[s * ROWS : (s + 1) * ROWS, :]
+            )

@@ -125,24 +125,21 @@ def tile_hydraattention_pa_kernel(tc, x, mask, W_kv_words, W_kv_scales, b_kv, ou
                 in_=grouped[:].rearrange("p w j -> p (w j)"),
             )
 
-        def project(t):
+        def project_bank(t, n):
             c, part = divmod(t, CHUNK_TILES)
-            banks = []
-            for n in range(BANKS_PER_TILE):
-                acc = psum.tile([P, BANK], F32, tag="acc")
-                for g in range(PASSES):
-                    px = slice(g * CHUNK + part * P, g * CHUNK + (part + 1) * P)
-                    nc.tensor.matmul_mx(
-                        out=acc[:],
-                        lhsT=x_codes[:, c, px].bitcast(FP8X4),
-                        lhsT_scale=x_scales[:, c, px],
-                        rhs=w_words[:, g, 2 * n * BANK : 2 * (n + 1) * BANK].bitcast(FP4X4),
-                        rhs_scale=w_planes[:, g, n * BANK : (n + 1) * BANK],
-                        start=(g == 0),
-                        stop=(g == PASSES - 1),
-                    )
-                banks.append(acc)
-            return banks
+            acc = psum.tile([P, BANK], F32, tag="acc")
+            for g in range(PASSES):
+                px = slice(g * CHUNK + part * P, g * CHUNK + (part + 1) * P)
+                nc.tensor.matmul_mx(
+                    out=acc[:],
+                    lhsT=x_codes[:, c, px].bitcast(FP8X4),
+                    lhsT_scale=x_scales[:, c, px],
+                    rhs=w_words[:, g, 2 * n * BANK : 2 * (n + 1) * BANK].bitcast(FP4X4),
+                    rhs_scale=w_planes[:, g, n * BANK : (n + 1) * BANK],
+                    start=(g == 0),
+                    stop=(g == PASSES - 1),
+                )
+            return acc
 
         def multiply(t, banks):
             kb = work.tile([P, CHANNELS], F32)
@@ -156,30 +153,29 @@ def tile_hydraattention_pa_kernel(tc, x, mask, W_kv_words, W_kv_scales, b_kv, ou
                     out=dst[:, cols], in0=banks[n][:], in1=bias[:, n * BANK : (n + 1) * BANK], op=ADD
                 )
             nc.scalar.activation(out=squares[:], in_=kb[:], func=ACT.Square, accum_out=sumsq[:, t : t + 1])
-            nc.gpsimd.tensor_tensor(out=prod[:], in0=kb[:], in1=vb[:], op=MULT)
+            nc.scalar.sqrt(out=norm[:, t : t + 1], in_=sumsq[:, t : t + 1])
+            nc.vector.tensor_tensor(out=prod[:], in0=kb[:], in1=vb[:], op=MULT)
             return prod
 
         def weigh(t):
-            nc.scalar.sqrt(out=norm[:, t : t + 1], in_=sumsq[:, t : t + 1])
             nc.vector.reciprocal(out=inv_norm[:, t : t + 1], in_=norm[:, t : t + 1])
             nc.vector.tensor_scalar(
                 out=weights[:, t, :], in0=mask_pair[:, t, :], scalar1=inv_norm[:, t : t + 1], scalar2=None, op0=MULT
             )
 
-        def pool_pixels(t, prod):
-            for j in range(BLOCKS):
-                nc.tensor.matmul(
-                    out=pooled[:, t, j, :],
-                    lhsT=prod[:, j * P : (j + 1) * P],
-                    rhs=weights[:, t, :],
-                    start=True,
-                    stop=True,
-                )
+        def pool_block(t, j, prod):
+            nc.tensor.matmul(
+                out=pooled[:, t, j, :],
+                lhsT=prod[:, j * P : (j + 1) * P],
+                rhs=weights[:, t, :],
+                start=True,
+                stop=True,
+            )
 
         grouped_of = {}
         quantise(0, regroup(nc.vector.tensor_copy, 0))
         grouped_of[1] = regroup(nc.scalar.copy, 1)
-        banks = project(0)
+        banks = [project_bank(0, n) for n in range(BANKS_PER_TILE)]
 
         nc.scalar.copy(out=mask_f32[:], in_=mask_rows[:])
         mask_cols = psum.tile([P, BANK], F32, tag="acc")
@@ -189,14 +185,18 @@ def tile_hydraattention_pa_kernel(tc, x, mask, W_kv_words, W_kv_scales, b_kv, ou
 
         prod_of = {}
         for t in range(TILES + 1):
-            if t + 1 < TILES:
-                upcoming = project(t + 1)
-            if t < TILES:
-                prod_of[t] = multiply(t, banks)
-                banks = upcoming
             if t >= 1:
                 weigh(t - 1)
-                pool_pixels(t - 1, prod_of[t - 1])
+            upcoming = []
+            for n in range(BANKS_PER_TILE):
+                if t + 1 < TILES:
+                    upcoming.append(project_bank(t + 1, n))
+                if t >= 1:
+                    for j in range(n * BLOCKS // BANKS_PER_TILE, (n + 1) * BLOCKS // BANKS_PER_TILE):
+                        pool_block(t - 1, j, prod_of[t - 1])
+            if t < TILES:
+                prod_of[t] = multiply(t, banks)
+            banks = upcoming
             if (t + 3) % CHUNK_TILES == 0 and t + 3 < TILES:
                 grouped_of[(t + 3) // CHUNK_TILES] = regroup(nc.scalar.copy, (t + 3) // CHUNK_TILES)
             if (t + 2) % CHUNK_TILES == 0 and t + 2 < TILES:

@@ -35,6 +35,7 @@ CHUNKS_PER_IMAGE = PIXELS // CHUNK
 BLOCKS = CHANNELS // P
 SUMS = 2
 ROWS = IMAGES * BLOCKS
+POOL_LAG = 2
 
 FLOPS = 2 * IMAGES * PIXELS * CHANNELS * KV
 
@@ -45,7 +46,7 @@ def tile_hydraattention_pa_kernel(tc, x, mask, W_kv_words, W_kv_scales, b_kv, ou
         keep = ctx.enter_context(tc.tile_pool(name="keep", bufs=1))
         stage = ctx.enter_context(tc.tile_pool(name="stage", bufs=2))
         work = ctx.enter_context(tc.tile_pool(name="work", bufs=3))
-        prods = ctx.enter_context(tc.tile_pool(name="prods", bufs=4))
+        prods = ctx.enter_context(tc.tile_pool(name="prods", bufs=5))
         psum = ctx.enter_context(tc.psum_pool(name="psum", bufs=7))
         psum_sums = ctx.enter_context(tc.psum_pool(name="psum_sums", bufs=1))
         ctx.enter_context(tc.manual_schedule())
@@ -61,18 +62,15 @@ def tile_hydraattention_pa_kernel(tc, x, mask, W_kv_words, W_kv_scales, b_kv, ou
         mask_f32 = keep.tile([P, P], F32)
         mask_pair = keep.tile([P, TILES, SUMS], F32)
         sumsq = keep.tile([P, TILES], F32)
-        norm = keep.tile([P, TILES], F32)
         inv_norm = keep.tile([P, TILES], F32)
         weights = keep.tile([P, TILES, SUMS], F32)
         sums = keep.tile([P, P], F32)
         rows = keep.tile([P, P], F32)
-        one = keep.tile([P, 1], F32)
-        one_root = keep.tile([P, 1], F32)
+        minus_half = keep.tile([P, 1], F32)
         pooled = psum_sums.tile([P, TILES, BLOCKS, SUMS], F32)
 
         nc.vector.memset(w_planes[:].rearrange("p g n -> p (g n)").bitcast(I32), 0)
-        nc.vector.memset(one[:], 1.0)
-        nc.scalar.sqrt(out=one_root[:], in_=one[:])
+        nc.vector.memset(minus_half[:], -0.5)
         nc.gpsimd.memset(mask_rows[:], 0.0)
         nc.gpsimd.memset(sums[:], 0.0)
         make_identity(nc, ident[:])
@@ -153,14 +151,20 @@ def tile_hydraattention_pa_kernel(tc, x, mask, W_kv_words, W_kv_scales, b_kv, ou
                     out=dst[:, cols], in0=banks[n][:], in1=bias[:, n * BANK : (n + 1) * BANK], op=ADD
                 )
             nc.scalar.activation(out=squares[:], in_=kb[:], func=ACT.Square, accum_out=sumsq[:, t : t + 1])
-            nc.scalar.sqrt(out=norm[:, t : t + 1], in_=sumsq[:, t : t + 1])
-            nc.vector.tensor_tensor(out=prod[:], in0=kb[:], in1=vb[:], op=MULT)
+            nc.gpsimd.tensor_tensor(out=prod[:], in0=kb[:], in1=vb[:], op=MULT)
             return prod
 
         def weigh(t):
-            nc.vector.reciprocal(out=inv_norm[:, t : t + 1], in_=norm[:, t : t + 1])
-            nc.vector.tensor_scalar(
-                out=weights[:, t, :], in0=mask_pair[:, t, :], scalar1=inv_norm[:, t : t + 1], scalar2=None, op0=MULT
+            nc.gpsimd.tensor_tensor(
+                out=inv_norm[:, t : t + 1], in0=sumsq[:, t : t + 1], in1=minus_half[:], op=mybir.AluOpType.pow
+            )
+            nc.gpsimd.tensor_scalar(
+                out=weights[:, t, :],
+                in0=mask_pair[:, t, :],
+                scalar1=inv_norm[:, t : t + 1],
+                scalar2=0.0,
+                op0=MULT,
+                op1=ADD,
             )
 
         def pool_block(t, j, prod):
@@ -184,16 +188,15 @@ def tile_hydraattention_pa_kernel(tc, x, mask, W_kv_words, W_kv_scales, b_kv, ou
         nc.scalar.copy(out=mask_pair[:, :, 1], in_=mask_cols[:, 0:TILES])
 
         prod_of = {}
-        for t in range(TILES + 1):
-            if t >= 1:
+        for t in range(TILES + POOL_LAG):
+            if 1 <= t <= TILES:
                 weigh(t - 1)
             upcoming = []
-            for n in range(BANKS_PER_TILE):
-                if t + 1 < TILES:
-                    upcoming.append(project_bank(t + 1, n))
-                if t >= 1:
-                    for j in range(n * BLOCKS // BANKS_PER_TILE, (n + 1) * BLOCKS // BANKS_PER_TILE):
-                        pool_block(t - 1, j, prod_of[t - 1])
+            if t + 1 < TILES:
+                upcoming = [project_bank(t + 1, n) for n in range(BANKS_PER_TILE)]
+            if t >= POOL_LAG:
+                for j in range(BLOCKS):
+                    pool_block(t - POOL_LAG, j, prod_of[t - POOL_LAG])
             if t < TILES:
                 prod_of[t] = multiply(t, banks)
             banks = upcoming

@@ -32,10 +32,7 @@ CHUNK_TILES = 2
 CHUNK = CHUNK_TILES * P
 CHUNKS = TILES // CHUNK_TILES
 CHUNKS_PER_IMAGE = PIXELS // CHUNK
-BLOCKS = CHANNELS // P
 SUMS = 2
-ROWS = IMAGES * BLOCKS
-POOL_LAG = 2
 
 FLOPS = 2 * IMAGES * PIXELS * CHANNELS * KV
 
@@ -46,8 +43,8 @@ def tile_hydraattention_pa_kernel(tc, x, mask, W_kv_words, W_kv_scales, b_kv, ou
         keep = ctx.enter_context(tc.tile_pool(name="keep", bufs=1))
         stage = ctx.enter_context(tc.tile_pool(name="stage", bufs=2))
         work = ctx.enter_context(tc.tile_pool(name="work", bufs=3))
-        prods = ctx.enter_context(tc.tile_pool(name="prods", bufs=5))
-        psum = ctx.enter_context(tc.psum_pool(name="psum", bufs=7))
+        prods = ctx.enter_context(tc.tile_pool(name="prods", bufs=4))
+        psum = ctx.enter_context(tc.psum_pool(name="psum", bufs=6))
         psum_sums = ctx.enter_context(tc.psum_pool(name="psum_sums", bufs=1))
         ctx.enter_context(tc.manual_schedule())
 
@@ -63,17 +60,15 @@ def tile_hydraattention_pa_kernel(tc, x, mask, W_kv_words, W_kv_scales, b_kv, ou
         mask_pair = keep.tile([P, TILES, SUMS], F32)
         sumsq = keep.tile([P, TILES], F32)
         inv_norm = keep.tile([P, TILES], F32)
-        weights = keep.tile([P, TILES, SUMS], F32)
-        sums = keep.tile([P, P], F32)
-        rows = keep.tile([P, P], F32)
         minus_half = keep.tile([P, 1], F32)
-        pooled = psum_sums.tile([P, TILES, BLOCKS, SUMS], F32)
+        weights = keep.tile([P, TILES, P], F32)
+        sums = keep.tile([P, IMAGES, CHANNELS], F32)
 
         nc.vector.memset(w_planes[:].rearrange("p g n -> p (g n)").bitcast(I32), 0)
         nc.vector.memset(minus_half[:], -0.5)
         nc.gpsimd.memset(mask_rows[:], 0.0)
-        nc.gpsimd.memset(sums[:], 0.0)
         make_identity(nc, ident[:])
+        nc.gpsimd.memset(weights[:], 0.0)
 
         x_rows = x.rearrange("b (g p j) h w -> b g p j (h w)", g=PASSES, p=P, j=PACK)
 
@@ -151,7 +146,7 @@ def tile_hydraattention_pa_kernel(tc, x, mask, W_kv_words, W_kv_scales, b_kv, ou
                     out=dst[:, cols], in0=banks[n][:], in1=bias[:, n * BANK : (n + 1) * BANK], op=ADD
                 )
             nc.scalar.activation(out=squares[:], in_=kb[:], func=ACT.Square, accum_out=sumsq[:, t : t + 1])
-            nc.gpsimd.tensor_tensor(out=prod[:], in0=kb[:], in1=vb[:], op=MULT)
+            nc.vector.tensor_tensor(out=prod[:], in0=kb[:], in1=vb[:], op=MULT)
             return prod
 
         def weigh(t):
@@ -159,7 +154,7 @@ def tile_hydraattention_pa_kernel(tc, x, mask, W_kv_words, W_kv_scales, b_kv, ou
                 out=inv_norm[:, t : t + 1], in0=sumsq[:, t : t + 1], in1=minus_half[:], op=mybir.AluOpType.pow
             )
             nc.gpsimd.tensor_scalar(
-                out=weights[:, t, :],
+                out=weights[:, t, 0:SUMS],
                 in0=mask_pair[:, t, :],
                 scalar1=inv_norm[:, t : t + 1],
                 scalar2=0.0,
@@ -167,14 +162,16 @@ def tile_hydraattention_pa_kernel(tc, x, mask, W_kv_words, W_kv_scales, b_kv, ou
                 op1=ADD,
             )
 
-        def pool_block(t, j, prod):
-            nc.tensor.matmul(
-                out=pooled[:, t, j, :],
-                lhsT=prod[:, j * P : (j + 1) * P],
-                rhs=weights[:, t, :],
-                start=True,
-                stop=True,
-            )
+        def pool_pixels(t, prod, pooled):
+            i = t % TILES_PER_IMAGE
+            for h in range(KEY_BANKS):
+                nc.tensor.matmul(
+                    out=pooled[h][:],
+                    lhsT=weights[:, t, :],
+                    rhs=prod[:, h * BANK : (h + 1) * BANK],
+                    start=(i == 0),
+                    stop=(i == TILES_PER_IMAGE - 1),
+                )
 
         grouped_of = {}
         quantise(0, regroup(nc.vector.tensor_copy, 0))
@@ -188,15 +185,21 @@ def tile_hydraattention_pa_kernel(tc, x, mask, W_kv_words, W_kv_scales, b_kv, ou
         nc.scalar.copy(out=mask_pair[:, :, 1], in_=mask_cols[:, 0:TILES])
 
         prod_of = {}
-        for t in range(TILES + POOL_LAG):
-            if 1 <= t <= TILES:
+        pooled = []
+        for t in range(TILES + 1):
+            if t >= 1:
                 weigh(t - 1)
             upcoming = []
             if t + 1 < TILES:
                 upcoming = [project_bank(t + 1, n) for n in range(BANKS_PER_TILE)]
-            if t >= POOL_LAG:
-                for j in range(BLOCKS):
-                    pool_block(t - POOL_LAG, j, prod_of[t - POOL_LAG])
+            if t >= 1:
+                b, i = divmod(t - 1, TILES_PER_IMAGE)
+                if i == 0:
+                    pooled = [psum_sums.tile([P, BANK], F32, name="pooled%d" % h) for h in range(KEY_BANKS)]
+                pool_pixels(t - 1, prod_of[t - 1], pooled)
+                if i == TILES_PER_IMAGE - 1:
+                    for h in range(KEY_BANKS):
+                        nc.scalar.copy(out=sums[0:32, b, h * BANK : (h + 1) * BANK], in_=pooled[h][0:32, :])
             if t < TILES:
                 prod_of[t] = multiply(t, banks)
             banks = upcoming
@@ -205,18 +208,5 @@ def tile_hydraattention_pa_kernel(tc, x, mask, W_kv_words, W_kv_scales, b_kv, ou
             if (t + 2) % CHUNK_TILES == 0 and t + 2 < TILES:
                 quantise((t + 2) // CHUNK_TILES, grouped_of[(t + 2) // CHUNK_TILES])
 
-        by_sum = pooled[:].rearrange("p (b i) j s -> p s b j i", b=IMAGES)
-        for s in range(SUMS):
-            nc.vector.tensor_reduce(
-                out=sums[:, s * ROWS : (s + 1) * ROWS].rearrange("p (b j) -> p b j", b=IMAGES),
-                in_=by_sum[:, s],
-                axis=mybir.AxisListType.X,
-                op=ADD,
-            )
-        turned = psum.tile([P, BANK], F32, tag="acc")
-        nc.tensor.transpose(out=turned[:, 0:P], in_=sums[:], identity=ident[:])
-        nc.vector.tensor_copy(out=rows[:], in_=turned[:, 0:P])
         for s, out in enumerate((out_0, out_1)):
-            nc.sync.dma_start(
-                out=out.rearrange("b o (j n) -> (b o j) n", n=P), in_=rows[s * ROWS : (s + 1) * ROWS, :]
-            )
+            nc.sync.dma_start(out=out.rearrange("b o n -> o b n"), in_=sums[s : s + 1, :, :])

@@ -32,7 +32,10 @@ CHUNK_TILES = 2
 CHUNK = CHUNK_TILES * P
 CHUNKS = TILES // CHUNK_TILES
 CHUNKS_PER_IMAGE = PIXELS // CHUNK
+BLOCKS = CHANNELS // P
 SUMS = 2
+ROWS = IMAGES * BLOCKS
+POOL_LAG = 2
 
 FLOPS = 2 * IMAGES * PIXELS * CHANNELS * KV
 
@@ -43,8 +46,8 @@ def tile_hydraattention_pa_kernel(tc, x, mask, W_kv_words, W_kv_scales, b_kv, ou
         keep = ctx.enter_context(tc.tile_pool(name="keep", bufs=1))
         stage = ctx.enter_context(tc.tile_pool(name="stage", bufs=2))
         work = ctx.enter_context(tc.tile_pool(name="work", bufs=3))
-        prods = ctx.enter_context(tc.tile_pool(name="prods", bufs=4))
-        psum = ctx.enter_context(tc.psum_pool(name="psum", bufs=6))
+        prods = ctx.enter_context(tc.tile_pool(name="prods", bufs=5))
+        psum = ctx.enter_context(tc.psum_pool(name="psum", bufs=7))
         psum_sums = ctx.enter_context(tc.psum_pool(name="psum_sums", bufs=1))
         ctx.enter_context(tc.manual_schedule())
 
@@ -60,15 +63,19 @@ def tile_hydraattention_pa_kernel(tc, x, mask, W_kv_words, W_kv_scales, b_kv, ou
         mask_pair = keep.tile([P, TILES, SUMS], F32)
         sumsq = keep.tile([P, TILES], F32)
         inv_norm = keep.tile([P, TILES], F32)
-        minus_half = keep.tile([P, 1], F32)
-        weights = keep.tile([P, TILES, P], F32)
-        sums = keep.tile([P, IMAGES, CHANNELS], F32)
+        weights = keep.tile([P, TILES, SUMS], F32)
+        sums = keep.tile([P, P], F32)
+        rows = keep.tile([P, P], F32)
+        one = keep.tile([P, 1], F32)
+        one_root = keep.tile([P, 1], F32)
+        pooled = psum_sums.tile([P, TILES, BLOCKS, SUMS], F32)
 
         nc.vector.memset(w_planes[:].rearrange("p g n -> p (g n)").bitcast(I32), 0)
-        nc.vector.memset(minus_half[:], -0.5)
+        nc.vector.memset(one[:], 1.0)
+        nc.scalar.activation(out=one_root[:], in_=one[:], func=ACT.Abs_reciprocal_sqrt)
         nc.gpsimd.memset(mask_rows[:], 0.0)
+        nc.gpsimd.memset(sums[:], 0.0)
         make_identity(nc, ident[:])
-        nc.gpsimd.memset(weights[:], 0.0)
 
         x_rows = x.rearrange("b (g p j) h w -> b g p j (h w)", g=PASSES, p=P, j=PACK)
 
@@ -146,32 +153,23 @@ def tile_hydraattention_pa_kernel(tc, x, mask, W_kv_words, W_kv_scales, b_kv, ou
                     out=dst[:, cols], in0=banks[n][:], in1=bias[:, n * BANK : (n + 1) * BANK], op=ADD
                 )
             nc.scalar.activation(out=squares[:], in_=kb[:], func=ACT.Square, accum_out=sumsq[:, t : t + 1])
-            nc.vector.tensor_tensor(out=prod[:], in0=kb[:], in1=vb[:], op=MULT)
+            nc.gpsimd.tensor_tensor(out=prod[:], in0=kb[:], in1=vb[:], op=MULT)
             return prod
 
         def weigh(t):
-            nc.gpsimd.tensor_tensor(
-                out=inv_norm[:, t : t + 1], in0=sumsq[:, t : t + 1], in1=minus_half[:], op=mybir.AluOpType.pow
-            )
-            nc.gpsimd.tensor_scalar(
-                out=weights[:, t, 0:SUMS],
-                in0=mask_pair[:, t, :],
-                scalar1=inv_norm[:, t : t + 1],
-                scalar2=0.0,
-                op0=MULT,
-                op1=ADD,
+            nc.scalar.activation(out=inv_norm[:, t : t + 1], in_=sumsq[:, t : t + 1], func=ACT.Abs_reciprocal_sqrt)
+            nc.scalar.activation(
+                out=weights[:, t, :], in_=mask_pair[:, t, :], func=ACT.Copy, scale=inv_norm[:, t : t + 1]
             )
 
-        def pool_pixels(t, prod, pooled):
-            i = t % TILES_PER_IMAGE
-            for h in range(KEY_BANKS):
-                nc.tensor.matmul(
-                    out=pooled[h][:],
-                    lhsT=weights[:, t, :],
-                    rhs=prod[:, h * BANK : (h + 1) * BANK],
-                    start=(i == 0),
-                    stop=(i == TILES_PER_IMAGE - 1),
-                )
+        def pool_block(t, j, prod):
+            nc.tensor.matmul(
+                out=pooled[:, t, j, :],
+                lhsT=prod[:, j * P : (j + 1) * P],
+                rhs=weights[:, t, :],
+                start=True,
+                stop=True,
+            )
 
         grouped_of = {}
         quantise(0, regroup(nc.vector.tensor_copy, 0))
@@ -185,21 +183,15 @@ def tile_hydraattention_pa_kernel(tc, x, mask, W_kv_words, W_kv_scales, b_kv, ou
         nc.scalar.copy(out=mask_pair[:, :, 1], in_=mask_cols[:, 0:TILES])
 
         prod_of = {}
-        pooled = []
-        for t in range(TILES + 1):
-            if t >= 1:
+        for t in range(TILES + POOL_LAG):
+            if 1 <= t <= TILES:
                 weigh(t - 1)
             upcoming = []
             if t + 1 < TILES:
                 upcoming = [project_bank(t + 1, n) for n in range(BANKS_PER_TILE)]
-            if t >= 1:
-                b, i = divmod(t - 1, TILES_PER_IMAGE)
-                if i == 0:
-                    pooled = [psum_sums.tile([P, BANK], F32, name="pooled%d" % h) for h in range(KEY_BANKS)]
-                pool_pixels(t - 1, prod_of[t - 1], pooled)
-                if i == TILES_PER_IMAGE - 1:
-                    for h in range(KEY_BANKS):
-                        nc.scalar.copy(out=sums[0:32, b, h * BANK : (h + 1) * BANK], in_=pooled[h][0:32, :])
+            if t >= POOL_LAG:
+                for j in range(BLOCKS):
+                    pool_block(t - POOL_LAG, j, prod_of[t - POOL_LAG])
             if t < TILES:
                 prod_of[t] = multiply(t, banks)
             banks = upcoming
@@ -208,5 +200,18 @@ def tile_hydraattention_pa_kernel(tc, x, mask, W_kv_words, W_kv_scales, b_kv, ou
             if (t + 2) % CHUNK_TILES == 0 and t + 2 < TILES:
                 quantise((t + 2) // CHUNK_TILES, grouped_of[(t + 2) // CHUNK_TILES])
 
+        by_sum = pooled[:].rearrange("p (b i) j s -> p s b j i", b=IMAGES)
+        for s in range(SUMS):
+            nc.vector.tensor_reduce(
+                out=sums[:, s * ROWS : (s + 1) * ROWS].rearrange("p (b j) -> p b j", b=IMAGES),
+                in_=by_sum[:, s],
+                axis=mybir.AxisListType.X,
+                op=ADD,
+            )
+        turned = psum.tile([P, BANK], F32, tag="acc")
+        nc.tensor.transpose(out=turned[:, 0:P], in_=sums[:], identity=ident[:])
+        nc.vector.tensor_copy(out=rows[:], in_=turned[:, 0:P])
         for s, out in enumerate((out_0, out_1)):
-            nc.sync.dma_start(out=out.rearrange("b o n -> o b n"), in_=sums[s : s + 1, :, :])
+            nc.sync.dma_start(
+                out=out.rearrange("b o (j n) -> (b o j) n", n=P), in_=rows[s * ROWS : (s + 1) * ROWS, :]
+            )

@@ -35,7 +35,6 @@ CHUNKS_PER_IMAGE = PIXELS // CHUNK
 BLOCKS = CHANNELS // P
 SUMS = 2
 ROWS = IMAGES * BLOCKS
-POOL_LAG = 2
 
 FLOPS = 2 * IMAGES * PIXELS * CHANNELS * KV
 
@@ -45,8 +44,8 @@ def tile_hydraattention_pa_kernel(tc, x, mask, W_kv_words, W_kv_scales, b_kv, ou
     with ExitStack() as ctx:
         keep = ctx.enter_context(tc.tile_pool(name="keep", bufs=1))
         stage = ctx.enter_context(tc.tile_pool(name="stage", bufs=2))
-        work = ctx.enter_context(tc.tile_pool(name="work", bufs=3))
-        prods = ctx.enter_context(tc.tile_pool(name="prods", bufs=5))
+        work = ctx.enter_context(tc.tile_pool(name="work", bufs=4))
+        prods = ctx.enter_context(tc.tile_pool(name="prods", bufs=4))
         psum = ctx.enter_context(tc.psum_pool(name="psum", bufs=7))
         psum_sums = ctx.enter_context(tc.psum_pool(name="psum_sums", bufs=1))
         ctx.enter_context(tc.manual_schedule())
@@ -56,6 +55,8 @@ def tile_hydraattention_pa_kernel(tc, x, mask, W_kv_words, W_kv_scales, b_kv, ou
         x_scales = keep.tile([P, CHUNKS, PASSES * CHUNK], U8, align_bytes=64)
         w_words = keep.tile([P, PASSES, 2 * KV], U8, align_bytes=64)
         w_planes = keep.tile([P, PASSES, KV], U8, align_bytes=64)
+        bias_row = keep.tile([P, KV], BF16)
+        ones = keep.tile([P, P], BF16)
         bias = keep.tile([P, KV], BF16)
         ident = keep.tile([P, P], F32)
         mask_rows = keep.tile([P, P], BF16)
@@ -70,7 +71,10 @@ def tile_hydraattention_pa_kernel(tc, x, mask, W_kv_words, W_kv_scales, b_kv, ou
         one_root = keep.tile([P, 1], F32)
         pooled = psum_sums.tile([P, TILES, BLOCKS, SUMS], F32)
 
+        nc.vector.memset(bias_row[:].bitcast(I32), 0)
+        nc.scalar.dma_start(out=bias_row[0:1, :], in_=b_kv.rearrange("(o n) -> o n", o=1))
         nc.vector.memset(w_planes[:].rearrange("p g n -> p (g n)").bitcast(I32), 0)
+        nc.vector.memset(ones[:], 1.0)
         nc.vector.memset(one[:], 1.0)
         nc.scalar.activation(out=one_root[:], in_=one[:], func=ACT.Abs_reciprocal_sqrt)
         nc.gpsimd.memset(mask_rows[:], 0.0)
@@ -100,7 +104,6 @@ def tile_hydraattention_pa_kernel(tc, x, mask, W_kv_words, W_kv_scales, b_kv, ou
                 out=w_planes[r:P:32, :, :].bitcast(I32),
                 in_=W_kv_scales[:, r : 4 * PACK : PACK, :].rearrange("g q n -> q g n").bitcast(I32),
             )
-        nc.sync.dma_start(out=bias[:], in_=b_kv.partition_broadcast(P))
         load_words(KV, 2 * KV)
         load_chunk(1)
         nc.sync.dma_start(
@@ -125,56 +128,73 @@ def tile_hydraattention_pa_kernel(tc, x, mask, W_kv_words, W_kv_scales, b_kv, ou
                 in_=grouped[:].rearrange("p w j -> p (w j)"),
             )
 
-        def project_bank(t, n):
-            c, part = divmod(t, CHUNK_TILES)
-            acc = psum.tile([P, BANK], F32, tag="acc")
-            for g in range(PASSES):
-                px = slice(g * CHUNK + part * P, g * CHUNK + (part + 1) * P)
-                nc.tensor.matmul_mx(
-                    out=acc[:],
-                    lhsT=x_codes[:, c, px].bitcast(FP8X4),
-                    lhsT_scale=x_scales[:, c, px],
-                    rhs=w_words[:, g, 2 * n * BANK : 2 * (n + 1) * BANK].bitcast(FP4X4),
-                    rhs_scale=w_planes[:, g, n * BANK : (n + 1) * BANK],
-                    start=(g == 0),
-                    stop=(g == PASSES - 1),
-                )
-            return acc
-
-        def multiply(t, banks):
-            kb = work.tile([P, CHANNELS], F32)
-            vb = work.tile([P, CHANNELS], F32)
-            squares = work.tile([P, CHANNELS], F32)
-            prod = prods.tile([P, CHANNELS], F32)
-            for n in range(BANKS_PER_TILE):
-                dst = kb if n < KEY_BANKS else vb
-                cols = slice((n % KEY_BANKS) * BANK, (n % KEY_BANKS + 1) * BANK)
-                nc.vector.tensor_tensor(
-                    out=dst[:, cols], in0=banks[n][:], in1=bias[:, n * BANK : (n + 1) * BANK], op=ADD
-                )
-            nc.scalar.activation(out=squares[:], in_=kb[:], func=ACT.Square, accum_out=sumsq[:, t : t + 1])
-            nc.gpsimd.tensor_tensor(out=prod[:], in0=kb[:], in1=vb[:], op=MULT)
-            return prod
-
-        def weigh(t):
-            nc.scalar.activation(out=inv_norm[:, t : t + 1], in_=sumsq[:, t : t + 1], func=ACT.Abs_reciprocal_sqrt)
-            nc.scalar.activation(
-                out=weights[:, t, :], in_=mask_pair[:, t, :], func=ACT.Copy, scale=inv_norm[:, t : t + 1]
-            )
-
-        def pool_block(t, j, prod):
+        def pool_block(t, j):
             nc.tensor.matmul(
                 out=pooled[:, t, j, :],
-                lhsT=prod[:, j * P : (j + 1) * P],
+                lhsT=prod_of[t][:, j * P : (j + 1) * P],
                 rhs=weights[:, t, :],
                 start=True,
                 stop=True,
             )
 
+        def project_bank(t, n, pool_tile):
+            c, part = divmod(t, CHUNK_TILES)
+            acc = None
+            if t < TILES:
+                acc = psum.tile([P, BANK], F32, tag="acc")
+            for g in range(PASSES):
+                if t < TILES:
+                    px = slice(g * CHUNK + part * P, g * CHUNK + (part + 1) * P)
+                    nc.tensor.matmul_mx(
+                        out=acc[:],
+                        lhsT=x_codes[:, c, px].bitcast(FP8X4),
+                        lhsT_scale=x_scales[:, c, px],
+                        rhs=w_words[:, g, 2 * n * BANK : 2 * (n + 1) * BANK].bitcast(FP4X4),
+                        rhs_scale=w_planes[:, g, n * BANK : (n + 1) * BANK],
+                        start=(g == 0),
+                        stop=(g == PASSES - 1),
+                    )
+                if pool_tile >= 0:
+                    pool_block(pool_tile, n * PASSES + g)
+            return acc
+
+        def add_bias(banks, first_bank):
+            biased = work.tile([P, CHANNELS], F32)
+            for h in range(KEY_BANKS):
+                n = first_bank + h
+                nc.vector.tensor_tensor(
+                    out=biased[:, h * BANK : (h + 1) * BANK],
+                    in0=banks[h][:],
+                    in1=bias[:, n * BANK : (n + 1) * BANK],
+                    op=ADD,
+                )
+            return biased
+
+        def weigh(t, kb):
+            squares = work.tile([P, CHANNELS], F32)
+            nc.scalar.activation(out=squares[:], in_=kb[:], func=ACT.Square, accum_out=sumsq[:, t : t + 1])
+            nc.scalar.activation(out=inv_norm[:, t : t + 1], in_=sumsq[:, t : t + 1], func=ACT.Abs_reciprocal_sqrt)
+            nc.scalar.activation(
+                out=weights[:, t, :], in_=mask_pair[:, t, :], func=ACT.Copy, scale=inv_norm[:, t : t + 1]
+            )
+
+        def multiply(kb, vb):
+            prod = prods.tile([P, CHANNELS], F32)
+            nc.vector.tensor_tensor(out=prod[:], in0=kb[:], in1=vb[:], op=MULT)
+            return prod
+
+        for n in range(BANKS_PER_TILE):
+            spread = psum.tile([P, BANK], F32, tag="acc")
+            nc.tensor.matmul(
+                out=spread[:], lhsT=ones[:], rhs=bias_row[:, n * BANK : (n + 1) * BANK], start=True, stop=True
+            )
+            nc.scalar.copy(out=bias[:, n * BANK : (n + 1) * BANK], in_=spread[:])
         grouped_of = {}
         quantise(0, regroup(nc.vector.tensor_copy, 0))
         grouped_of[1] = regroup(nc.scalar.copy, 1)
-        banks = [project_bank(0, n) for n in range(BANKS_PER_TILE)]
+        prod_of = {}
+        key_banks = [project_bank(0, n, -1) for n in range(KEY_BANKS)]
+        value_banks = [project_bank(0, n, -1) for n in range(KEY_BANKS, BANKS_PER_TILE)]
 
         nc.scalar.copy(out=mask_f32[:], in_=mask_rows[:])
         mask_cols = psum.tile([P, BANK], F32, tag="acc")
@@ -182,36 +202,32 @@ def tile_hydraattention_pa_kernel(tc, x, mask, W_kv_words, W_kv_scales, b_kv, ou
         nc.scalar.activation(out=mask_pair[:, :, 0], in_=mask_cols[:, 0:TILES], func=ACT.Copy, scale=-1.0, bias=1.0)
         nc.scalar.copy(out=mask_pair[:, :, 1], in_=mask_cols[:, 0:TILES])
 
-        prod_of = {}
-        for t in range(TILES + POOL_LAG):
-            if 1 <= t <= TILES:
-                weigh(t - 1)
-            upcoming = []
-            if t + 1 < TILES:
-                upcoming = [project_bank(t + 1, n) for n in range(BANKS_PER_TILE)]
-            if t >= POOL_LAG:
-                for j in range(BLOCKS):
-                    pool_block(t - POOL_LAG, j, prod_of[t - POOL_LAG])
+        kb = vb = None
+        for t in range(TILES + 1):
+            last_kb = kb
             if t < TILES:
-                prod_of[t] = multiply(t, banks)
-            banks = upcoming
+                kb = add_bias(key_banks, 0)
+                weigh(t, kb)
+            if t >= 1:
+                prod_of[t - 1] = multiply(last_kb, vb)
+            next_banks = [project_bank(t + 1, n, t - 1) for n in range(BANKS_PER_TILE)]
+            if t < TILES:
+                vb = add_bias(value_banks, KEY_BANKS)
+            key_banks = next_banks[0:KEY_BANKS]
+            value_banks = next_banks[KEY_BANKS:BANKS_PER_TILE]
             if (t + 3) % CHUNK_TILES == 0 and t + 3 < TILES:
                 grouped_of[(t + 3) // CHUNK_TILES] = regroup(nc.scalar.copy, (t + 3) // CHUNK_TILES)
             if (t + 2) % CHUNK_TILES == 0 and t + 2 < TILES:
                 quantise((t + 2) // CHUNK_TILES, grouped_of[(t + 2) // CHUNK_TILES])
 
-        by_sum = pooled[:].rearrange("p (b i) j s -> p s b j i", b=IMAGES)
-        for s in range(SUMS):
-            nc.vector.tensor_reduce(
-                out=sums[:, s * ROWS : (s + 1) * ROWS].rearrange("p (b j) -> p b j", b=IMAGES),
-                in_=by_sum[:, s],
-                axis=mybir.AxisListType.X,
-                op=ADD,
-            )
+        nc.vector.tensor_reduce(
+            out=sums[:, 0 : SUMS * ROWS].rearrange("p (b q) -> p b q", b=IMAGES),
+            in_=pooled[:].rearrange("p (b i) j s -> p b (j s) i", b=IMAGES),
+            axis=mybir.AxisListType.X,
+            op=ADD,
+        )
         turned = psum.tile([P, BANK], F32, tag="acc")
         nc.tensor.transpose(out=turned[:, 0:P], in_=sums[:], identity=ident[:])
         nc.vector.tensor_copy(out=rows[:], in_=turned[:, 0:P])
         for s, out in enumerate((out_0, out_1)):
-            nc.sync.dma_start(
-                out=out.rearrange("b o (j n) -> (b o j) n", n=P), in_=rows[s * ROWS : (s + 1) * ROWS, :]
-            )
+            nc.sync.dma_start(out=out.rearrange("b o (j n) -> (b o j) n", n=P), in_=rows[s : SUMS * ROWS : SUMS, :])

@@ -202,23 +202,24 @@ def tile_hydraattention_pa_kernel(tc, x, mask, W_kv_words, W_kv_scales, b_kv, ou
         nc.scalar.activation(out=mask_pair[:, :, 0], in_=mask_cols[:, 0:TILES], func=ACT.Copy, scale=-1.0, bias=1.0)
         nc.scalar.copy(out=mask_pair[:, :, 1], in_=mask_cols[:, 0:TILES])
 
+        key_banks_of = {0: key_banks, 1: [project_bank(1, n, -1) for n in range(KEY_BANKS)]}
         kb = vb = None
         for t in range(TILES + 1):
             last_kb = kb
             if t < TILES:
-                kb = add_bias(key_banks, 0)
+                kb = add_bias(key_banks_of[t], 0)
                 weigh(t, kb)
             if t >= 1:
                 prod_of[t - 1] = multiply(last_kb, vb)
-            next_banks = [project_bank(t + 1, n, t - 1) for n in range(BANKS_PER_TILE)]
+            next_value_banks = [project_bank(t + 1, n, t - 1) for n in range(KEY_BANKS, BANKS_PER_TILE)]
             if t < TILES:
                 vb = add_bias(value_banks, KEY_BANKS)
-            key_banks = next_banks[0:KEY_BANKS]
-            value_banks = next_banks[KEY_BANKS:BANKS_PER_TILE]
+            value_banks = next_value_banks
             if (t + 3) % CHUNK_TILES == 0 and t + 3 < TILES:
                 grouped_of[(t + 3) // CHUNK_TILES] = regroup(nc.scalar.copy, (t + 3) // CHUNK_TILES)
             if (t + 2) % CHUNK_TILES == 0 and t + 2 < TILES:
                 quantise((t + 2) // CHUNK_TILES, grouped_of[(t + 2) // CHUNK_TILES])
+            key_banks_of[t + 2] = [project_bank(t + 2, n, t - 1) for n in range(KEY_BANKS)]
 
         nc.vector.tensor_reduce(
             out=sums[:, 0 : SUMS * ROWS].rearrange("p (b q) -> p b q", b=IMAGES),

@@ -23,6 +23,8 @@ P = 128
 PACK = 4
 K_PASS = P * PACK
 PASSES = CHANNELS // K_PASS
+SCALE_ROWS = K_PASS // 32
+QUADRANT = 32
 BANK = 512
 BANKS_PER_TILE = KV // BANK
 KEY_BANKS = CHANNELS // BANK
@@ -32,9 +34,15 @@ CHUNK_TILES = 2
 CHUNK = CHUNK_TILES * P
 CHUNKS = TILES // CHUNK_TILES
 CHUNKS_PER_IMAGE = PIXELS // CHUNK
-BLOCKS = CHANNELS // P
+RUN = 4
+STRIPS = CHANNELS // P
 SUMS = 2
-ROWS = IMAGES * BLOCKS
+ROWS = SUMS * IMAGES * STRIPS
+NO_TILE = -1
+REGROUP_AHEAD = 3
+QUANTISE_AHEAD = 2
+
+assert STRIPS == BANKS_PER_TILE * PASSES
 
 FLOPS = 2 * IMAGES * PIXELS * CHANNELS * KV
 
@@ -44,8 +52,9 @@ def tile_hydraattention_pa_kernel(tc, x, mask, W_kv_words, W_kv_scales, b_kv, ou
     with ExitStack() as ctx:
         keep = ctx.enter_context(tc.tile_pool(name="keep", bufs=1))
         stage = ctx.enter_context(tc.tile_pool(name="stage", bufs=2))
-        work = ctx.enter_context(tc.tile_pool(name="work", bufs=4))
-        prods = ctx.enter_context(tc.tile_pool(name="prods", bufs=4))
+        biased_pool = ctx.enter_context(tc.tile_pool(name="biased", bufs=4))
+        scratch = ctx.enter_context(tc.tile_pool(name="scratch", bufs=2))
+        prod_pool = ctx.enter_context(tc.tile_pool(name="prod", bufs=3))
         psum = ctx.enter_context(tc.psum_pool(name="psum", bufs=7))
         psum_sums = ctx.enter_context(tc.psum_pool(name="psum_sums", bufs=1))
         ctx.enter_context(tc.manual_schedule())
@@ -54,7 +63,7 @@ def tile_hydraattention_pa_kernel(tc, x, mask, W_kv_words, W_kv_scales, b_kv, ou
         x_codes = keep.tile([P, CHUNKS, PASSES * CHUNK], U32, align_bytes=64)
         x_scales = keep.tile([P, CHUNKS, PASSES * CHUNK], U8, align_bytes=64)
         w_words = keep.tile([P, PASSES, 2 * KV], U8, align_bytes=64)
-        w_planes = keep.tile([P, PASSES, KV], U8, align_bytes=64)
+        w_scales = keep.tile([P, PASSES, KV], U8, align_bytes=64)
         bias_row = keep.tile([P, KV], BF16)
         ones = keep.tile([P, P], BF16)
         bias = keep.tile([P, KV], BF16)
@@ -67,121 +76,129 @@ def tile_hydraattention_pa_kernel(tc, x, mask, W_kv_words, W_kv_scales, b_kv, ou
         weights = keep.tile([P, TILES, SUMS], F32)
         sums = keep.tile([P, P], F32)
         rows = keep.tile([P, P], F32)
-        one = keep.tile([P, 1], F32)
-        one_root = keep.tile([P, 1], F32)
-        pooled = psum_sums.tile([P, TILES, BLOCKS, SUMS], F32)
+        table_in = keep.tile([P, 1], F32)
+        table_out = keep.tile([P, 1], F32)
+        pooled = psum_sums.tile([P, TILES, STRIPS, SUMS], F32)
 
         nc.vector.memset(bias_row[:].bitcast(I32), 0)
-        nc.scalar.dma_start(out=bias_row[0:1, :], in_=b_kv.rearrange("(o n) -> o n", o=1))
-        nc.vector.memset(w_planes[:].rearrange("p g n -> p (g n)").bitcast(I32), 0)
+        nc.scalar.dma_start(out=bias_row[0:1, :], in_=b_kv.rearrange("(o kv) -> o kv", o=1))
+        nc.vector.memset(w_scales[:].rearrange("p g kv -> p (g kv)").bitcast(I32), 0)
         nc.vector.memset(ones[:], 1.0)
-        nc.vector.memset(one[:], 1.0)
-        nc.scalar.activation(out=one_root[:], in_=one[:], func=ACT.Abs_reciprocal_sqrt)
+        nc.vector.memset(table_in[:], 1.0)
+        nc.scalar.activation(out=table_out[:], in_=table_in[:], func=ACT.Abs_reciprocal_sqrt)
         nc.gpsimd.memset(mask_rows[:], 0.0)
         nc.gpsimd.memset(sums[:], 0.0)
         make_identity(nc, ident[:])
 
-        x_rows = x.rearrange("b (g p j) h w -> b g p j (h w)", g=PASSES, p=P, j=PACK)
+        x_rows = x.rearrange("b (g p j) row col -> b g p j (row col)", g=PASSES, p=P, j=PACK)
 
-        def load_chunk(c):
-            b, part = divmod(c, CHUNKS_PER_IMAGE)
+        def load_chunk(chunk):
+            b, quarter = divmod(chunk, CHUNKS_PER_IMAGE)
             for g in range(PASSES):
                 nc.sync.dma_start(
-                    out=raw[:, c, :, g * CHUNK : (g + 1) * CHUNK],
-                    in_=x_rows[b, g, :, :, part * CHUNK : (part + 1) * CHUNK],
+                    out=raw[:, chunk, :, g * CHUNK : (g + 1) * CHUNK],
+                    in_=x_rows[b, g, :, :, quarter * CHUNK : (quarter + 1) * CHUNK],
                 )
 
         def load_words(first_byte, last_byte):
             nc.sync.dma_start(
                 out=w_words[:, :, first_byte:last_byte].bitcast(I32),
-                in_=W_kv_words.rearrange("g p n -> p g n")[:, :, first_byte:last_byte].bitcast(I32),
+                in_=W_kv_words.rearrange("g p byte -> p g byte")[:, :, first_byte:last_byte].bitcast(I32),
             )
 
         load_chunk(0)
         load_words(0, KV)
         for r in range(PACK):
             nc.sync.dma_start(
-                out=w_planes[r:P:32, :, :].bitcast(I32),
-                in_=W_kv_scales[:, r : 4 * PACK : PACK, :].rearrange("g q n -> q g n").bitcast(I32),
+                out=w_scales[r:P:QUADRANT, :, :].bitcast(I32),
+                in_=W_kv_scales[:, r:SCALE_ROWS:PACK, :].rearrange("g q kv -> q g kv").bitcast(I32),
             )
         load_words(KV, 2 * KV)
         load_chunk(1)
         nc.sync.dma_start(
             out=mask_rows[0:TILES, :],
-            in_=mask.rearrange("b o (i r) w -> (b o i) (r w)", i=TILES_PER_IMAGE),
+            in_=mask.rearrange("b o (i row) col -> (b o i) (row col)", i=TILES_PER_IMAGE),
         )
-        for c in range(2, CHUNKS):
-            load_chunk(c)
+        for chunk in range(2, CHUNKS):
+            load_chunk(chunk)
 
-        def regroup(copy, c):
+        def regroup(copy, chunk):
             grouped = stage.tile([P, PASSES * CHUNK, PACK], BF16, align_bytes=64)
             copy(
-                out=grouped[:].rearrange("p (c i) j -> p c j i", i=4),
-                in_=raw[:, c].rearrange("p j (c i) -> p c j i", i=4),
+                out=grouped[:].rearrange("p (run e) j -> p run j e", e=RUN),
+                in_=raw[:, chunk].rearrange("p j (run e) -> p run j e", e=RUN),
             )
             return grouped
 
-        def quantise(c, grouped):
+        def quantise(chunk, grouped):
             nc.vector.quantize_mx(
-                out=x_codes[:, c, :].bitcast(FP8X4),
-                scales=x_scales[:, c, :],
-                in_=grouped[:].rearrange("p w j -> p (w j)"),
+                out=x_codes[:, chunk, :].bitcast(FP8X4),
+                scales=x_scales[:, chunk, :],
+                in_=grouped[:].rearrange("p px j -> p (px j)"),
             )
 
-        def pool_block(t, j):
+        def pool_strip(t, strip):
             nc.tensor.matmul(
-                out=pooled[:, t, j, :],
-                lhsT=prod_of[t][:, j * P : (j + 1) * P],
+                out=pooled[:, t, strip, :],
+                lhsT=prod_of[t][:, strip * P : (strip + 1) * P],
                 rhs=weights[:, t, :],
                 start=True,
                 stop=True,
             )
 
         def project_bank(t, n, pool_tile):
-            c, part = divmod(t, CHUNK_TILES)
+            chunk, place = divmod(t, CHUNK_TILES)
             acc = None
             if t < TILES:
                 acc = psum.tile([P, BANK], F32, tag="acc")
             for g in range(PASSES):
                 if t < TILES:
-                    px = slice(g * CHUNK + part * P, g * CHUNK + (part + 1) * P)
+                    pixels = slice(g * CHUNK + place * P, g * CHUNK + (place + 1) * P)
                     nc.tensor.matmul_mx(
                         out=acc[:],
-                        lhsT=x_codes[:, c, px].bitcast(FP8X4),
-                        lhsT_scale=x_scales[:, c, px],
+                        lhsT=x_codes[:, chunk, pixels].bitcast(FP8X4),
+                        lhsT_scale=x_scales[:, chunk, pixels],
                         rhs=w_words[:, g, 2 * n * BANK : 2 * (n + 1) * BANK].bitcast(FP4X4),
-                        rhs_scale=w_planes[:, g, n * BANK : (n + 1) * BANK],
+                        rhs_scale=w_scales[:, g, n * BANK : (n + 1) * BANK],
                         start=(g == 0),
                         stop=(g == PASSES - 1),
                     )
-                if pool_tile >= 0:
-                    pool_block(pool_tile, n * PASSES + g)
+                if pool_tile != NO_TILE:
+                    pool_strip(pool_tile, n * PASSES + g)
             return acc
 
-        def add_bias(banks, first_bank):
-            biased = work.tile([P, CHANNELS], F32)
-            for h in range(KEY_BANKS):
-                n = first_bank + h
-                nc.vector.tensor_tensor(
-                    out=biased[:, h * BANK : (h + 1) * BANK],
-                    in0=banks[h][:],
-                    in1=bias[:, n * BANK : (n + 1) * BANK],
-                    op=ADD,
-                )
+        def new_biased():
+            biased = biased_pool.tile([P, CHANNELS], F32)
             return biased
 
-        def weigh(t, kb):
-            squares = work.tile([P, CHANNELS], F32)
-            nc.scalar.activation(out=squares[:], in_=kb[:], func=ACT.Square, accum_out=sumsq[:, t : t + 1])
+        def add_bias(biased, banks, n):
+            h = n % KEY_BANKS
+            nc.vector.tensor_tensor(
+                out=biased[:, h * BANK : (h + 1) * BANK],
+                in0=banks[n][:],
+                in1=bias[:, n * BANK : (n + 1) * BANK],
+                op=ADD,
+            )
+
+        def weigh(t):
+            squares = scratch.tile([P, CHANNELS], F32)
+            nc.scalar.activation(out=squares[:], in_=keys_of[t][:], func=ACT.Square, accum_out=sumsq[:, t : t + 1])
             nc.scalar.activation(out=inv_norm[:, t : t + 1], in_=sumsq[:, t : t + 1], func=ACT.Abs_reciprocal_sqrt)
             nc.scalar.activation(
                 out=weights[:, t, :], in_=mask_pair[:, t, :], func=ACT.Copy, scale=inv_norm[:, t : t + 1]
             )
 
-        def multiply(kb, vb):
-            prod = prods.tile([P, CHANNELS], F32)
-            nc.vector.tensor_tensor(out=prod[:], in0=kb[:], in1=vb[:], op=MULT)
-            return prod
+        def multiply(t):
+            prod = prod_pool.tile([P, CHANNELS], F32)
+            nc.vector.tensor_tensor(out=prod[:], in0=keys_of[t][:], in1=values_of[t][:], op=MULT)
+            prod_of[t] = prod
+
+        def opens_chunk(t):
+            return t < TILES and t % CHUNK_TILES == 0
+
+        keys_of = {}
+        values_of = {}
+        prod_of = {}
 
         for n in range(BANKS_PER_TILE):
             spread = psum.tile([P, BANK], F32, tag="acc")
@@ -189,12 +206,9 @@ def tile_hydraattention_pa_kernel(tc, x, mask, W_kv_words, W_kv_scales, b_kv, ou
                 out=spread[:], lhsT=ones[:], rhs=bias_row[:, n * BANK : (n + 1) * BANK], start=True, stop=True
             )
             nc.scalar.copy(out=bias[:, n * BANK : (n + 1) * BANK], in_=spread[:])
-        grouped_of = {}
         quantise(0, regroup(nc.vector.tensor_copy, 0))
-        grouped_of[1] = regroup(nc.scalar.copy, 1)
-        prod_of = {}
-        key_banks = [project_bank(0, n, -1) for n in range(KEY_BANKS)]
-        value_banks = [project_bank(0, n, -1) for n in range(KEY_BANKS, BANKS_PER_TILE)]
+        grouped = regroup(nc.scalar.copy, 1)
+        banks = [project_bank(0, n, NO_TILE) for n in range(BANKS_PER_TILE)]
 
         nc.scalar.copy(out=mask_f32[:], in_=mask_rows[:])
         mask_cols = psum.tile([P, BANK], F32, tag="acc")
@@ -202,28 +216,31 @@ def tile_hydraattention_pa_kernel(tc, x, mask, W_kv_words, W_kv_scales, b_kv, ou
         nc.scalar.activation(out=mask_pair[:, :, 0], in_=mask_cols[:, 0:TILES], func=ACT.Copy, scale=-1.0, bias=1.0)
         nc.scalar.copy(out=mask_pair[:, :, 1], in_=mask_cols[:, 0:TILES])
 
-        key_banks_of = {0: key_banks, 1: [project_bank(1, n, -1) for n in range(KEY_BANKS)]}
-        kb = vb = None
         for t in range(TILES + 1):
-            last_kb = kb
             if t < TILES:
-                kb = add_bias(key_banks_of[t], 0)
-                weigh(t, kb)
+                keys_of[t] = new_biased()
+                add_bias(keys_of[t], banks, 0)
             if t >= 1:
-                prod_of[t - 1] = multiply(last_kb, vb)
-            next_value_banks = [project_bank(t + 1, n, t - 1) for n in range(KEY_BANKS, BANKS_PER_TILE)]
+                multiply(t - 1)
             if t < TILES:
-                vb = add_bias(value_banks, KEY_BANKS)
-            value_banks = next_value_banks
-            if (t + 3) % CHUNK_TILES == 0 and t + 3 < TILES:
-                grouped_of[(t + 3) // CHUNK_TILES] = regroup(nc.scalar.copy, (t + 3) // CHUNK_TILES)
-            if (t + 2) % CHUNK_TILES == 0 and t + 2 < TILES:
-                quantise((t + 2) // CHUNK_TILES, grouped_of[(t + 2) // CHUNK_TILES])
-            key_banks_of[t + 2] = [project_bank(t + 2, n, t - 1) for n in range(KEY_BANKS)]
+                for n in range(1, KEY_BANKS):
+                    add_bias(keys_of[t], banks, n)
+                weigh(t)
+            pool_tile = t - 1 if t >= 1 else NO_TILE
+            next_banks = [project_bank(t + 1, n, pool_tile) for n in range(BANKS_PER_TILE)]
+            if t < TILES:
+                values_of[t] = new_biased()
+                for n in range(KEY_BANKS, BANKS_PER_TILE):
+                    add_bias(values_of[t], banks, n)
+            banks = next_banks
+            if opens_chunk(t + REGROUP_AHEAD):
+                grouped = regroup(nc.scalar.copy, (t + REGROUP_AHEAD) // CHUNK_TILES)
+            if opens_chunk(t + QUANTISE_AHEAD):
+                quantise((t + QUANTISE_AHEAD) // CHUNK_TILES, grouped)
 
         nc.vector.tensor_reduce(
-            out=sums[:, 0 : SUMS * ROWS].rearrange("p (b q) -> p b q", b=IMAGES),
-            in_=pooled[:].rearrange("p (b i) j s -> p b (j s) i", b=IMAGES),
+            out=sums[:, 0:ROWS].rearrange("p (b rest) -> p b rest", b=IMAGES),
+            in_=pooled[:].rearrange("p (b i) strip s -> p b (strip s) i", b=IMAGES),
             axis=mybir.AxisListType.X,
             op=ADD,
         )
@@ -231,4 +248,4 @@ def tile_hydraattention_pa_kernel(tc, x, mask, W_kv_words, W_kv_scales, b_kv, ou
         nc.tensor.transpose(out=turned[:, 0:P], in_=sums[:], identity=ident[:])
         nc.vector.tensor_copy(out=rows[:], in_=turned[:, 0:P])
         for s, out in enumerate((out_0, out_1)):
-            nc.sync.dma_start(out=out.rearrange("b o (j n) -> (b o j) n", n=P), in_=rows[s : SUMS * ROWS : SUMS, :])
+            nc.sync.dma_start(out=out.rearrange("b o (strip ch) -> (b o strip) ch", ch=P), in_=rows[s:ROWS:SUMS, :])

@@ -52,7 +52,7 @@ def tile_hydraattention_pa_kernel(tc, x, mask, W_kv_words, W_kv_scales, b_kv, ou
     with ExitStack() as ctx:
         keep = ctx.enter_context(tc.tile_pool(name="keep", bufs=1))
         stage = ctx.enter_context(tc.tile_pool(name="stage", bufs=2))
-        biased_pool = ctx.enter_context(tc.tile_pool(name="biased", bufs=4))
+        biased_pool = ctx.enter_context(tc.tile_pool(name="biased", bufs=6))
         scratch = ctx.enter_context(tc.tile_pool(name="scratch", bufs=2))
         prod_pool = ctx.enter_context(tc.tile_pool(name="prod", bufs=3))
         psum = ctx.enter_context(tc.psum_pool(name="psum", bufs=7))
@@ -189,8 +189,11 @@ def tile_hydraattention_pa_kernel(tc, x, mask, W_kv_words, W_kv_scales, b_kv, ou
             )
 
         def multiply(t):
+            engine = nc.vector if t == TILES - 1 else nc.gpsimd
             prod = prod_pool.tile([P, CHANNELS], F32)
-            nc.vector.tensor_tensor(out=prod[:], in0=keys_of[t][:], in1=values_of[t][:], op=MULT)
+            for h in range(KEY_BANKS):
+                half = slice(h * BANK, (h + 1) * BANK)
+                engine.tensor_tensor(out=prod[:, half], in0=keys_of[t][:, half], in1=values_of[t][:, half], op=MULT)
             prod_of[t] = prod
 
         def opens_chunk(t):
@@ -219,20 +222,15 @@ def tile_hydraattention_pa_kernel(tc, x, mask, W_kv_words, W_kv_scales, b_kv, ou
         for t in range(TILES + 1):
             if t < TILES:
                 keys_of[t] = new_biased()
-                add_bias(keys_of[t], banks, 0)
-            if t >= 1:
-                multiply(t - 1)
-            if t < TILES:
-                for n in range(1, KEY_BANKS):
+                for n in range(KEY_BANKS):
                     add_bias(keys_of[t], banks, n)
                 weigh(t)
-            pool_tile = t - 1 if t >= 1 else NO_TILE
-            next_banks = [project_bank(t + 1, n, pool_tile) for n in range(BANKS_PER_TILE)]
-            if t < TILES:
                 values_of[t] = new_biased()
                 for n in range(KEY_BANKS, BANKS_PER_TILE):
                     add_bias(values_of[t], banks, n)
-            banks = next_banks
+                multiply(t)
+            pool_tile = t - 1 if t >= 1 else NO_TILE
+            banks = [project_bank(t + 1, n, pool_tile) for n in range(BANKS_PER_TILE)]
             if opens_chunk(t + REGROUP_AHEAD):
                 grouped = regroup(nc.scalar.copy, (t + REGROUP_AHEAD) // CHUNK_TILES)
             if opens_chunk(t + QUANTISE_AHEAD):

@@ -39,6 +39,8 @@ STRIPS = CHANNELS // P
 SUMS = 2
 ROWS = SUMS * IMAGES * STRIPS
 NO_TILE = -1
+ACC_STRIPS = 2
+ACC_WIDTH = ACC_STRIPS * P
 REGROUP_AHEAD = 3
 QUANTISE_AHEAD = 2
 
@@ -55,6 +57,7 @@ def tile_hydraattention_pa_kernel(tc, x, mask, W_kv_words, W_kv_scales, b_kv, ou
         biased_pool = ctx.enter_context(tc.tile_pool(name="biased", bufs=6))
         scratch = ctx.enter_context(tc.tile_pool(name="scratch", bufs=2))
         prod_pool = ctx.enter_context(tc.tile_pool(name="prod", bufs=3))
+        acc_pool = ctx.enter_context(tc.tile_pool(name="acc", bufs=4))
         psum = ctx.enter_context(tc.psum_pool(name="psum", bufs=7))
         psum_sums = ctx.enter_context(tc.psum_pool(name="psum_sums", bufs=1))
         ctx.enter_context(tc.manual_schedule())
@@ -76,6 +79,8 @@ def tile_hydraattention_pa_kernel(tc, x, mask, W_kv_words, W_kv_scales, b_kv, ou
         weights = keep.tile([P, TILES, SUMS], F32)
         sums = keep.tile([P, P], F32)
         rows = keep.tile([P, P], F32)
+        zeros = keep.tile([P, SUMS, ACC_WIDTH], F32)
+        one_col = keep.tile([P, 1], F32)
         table_in = keep.tile([P, 1], F32)
         table_out = keep.tile([P, 1], F32)
         pooled = psum_sums.tile([P, TILES, STRIPS, SUMS], F32)
@@ -88,6 +93,8 @@ def tile_hydraattention_pa_kernel(tc, x, mask, W_kv_words, W_kv_scales, b_kv, ou
         nc.scalar.activation(out=table_out[:], in_=table_in[:], func=ACT.Abs_reciprocal_sqrt)
         nc.gpsimd.memset(mask_rows[:], 0.0)
         nc.gpsimd.memset(sums[:], 0.0)
+        nc.gpsimd.memset(zeros[:], 0.0)
+        nc.gpsimd.memset(one_col[:], 1.0)
         make_identity(nc, ident[:])
 
         x_rows = x.rearrange("b (g p j) row col -> b g p j (row col)", g=PASSES, p=P, j=PACK)
@@ -146,6 +153,42 @@ def tile_hydraattention_pa_kernel(tc, x, mask, W_kv_words, W_kv_scales, b_kv, ou
                 stop=True,
             )
 
+        def pooled_directly(t):
+            return t % TILES_PER_IMAGE == TILES_PER_IMAGE - 1
+
+        def pool_running_sum(b, strip, s):
+            nc.tensor.matmul(
+                out=pooled[:, b * TILES_PER_IMAGE, strip, s : s + 1],
+                lhsT=acc_of[b][:, s, strip * P : (strip + 1) * P],
+                rhs=one_col[:],
+                start=True,
+                stop=True,
+            )
+
+        def place_behind_pass(pool_tile, strip):
+            if pool_tile != NO_TILE and (strip >= ACC_STRIPS or pooled_directly(pool_tile)):
+                pool_strip(pool_tile, strip)
+            elif served["count"] < len(waiting):
+                pool_running_sum(*waiting[served["count"]])
+                served["count"] += 1
+
+        def accumulate(t):
+            b, i = divmod(t, TILES_PER_IMAGE)
+            before = zeros if i == 0 else acc_of[b]
+            acc = acc_pool.tile([P, SUMS, ACC_WIDTH], F32)
+            for s in range(SUMS):
+                nc.vector.scalar_tensor_tensor(
+                    out=acc[:, s, :],
+                    in0=prod_of[t][:, 0:ACC_WIDTH],
+                    scalar=weights[:, t, s : s + 1],
+                    in1=before[:, s, :],
+                    op0=MULT,
+                    op1=ADD,
+                )
+            acc_of[b] = acc
+            if pooled_directly(t + 1):
+                waiting.extend((b, strip, s) for strip in range(ACC_STRIPS) for s in range(SUMS))
+
         def project_bank(t, n, pool_tile):
             chunk, place = divmod(t, CHUNK_TILES)
             acc = None
@@ -163,8 +206,7 @@ def tile_hydraattention_pa_kernel(tc, x, mask, W_kv_words, W_kv_scales, b_kv, ou
                         start=(g == 0),
                         stop=(g == PASSES - 1),
                     )
-                if pool_tile != NO_TILE:
-                    pool_strip(pool_tile, n * PASSES + g)
+                place_behind_pass(pool_tile, n * PASSES + g)
             return acc
 
         def new_biased():
@@ -191,9 +233,9 @@ def tile_hydraattention_pa_kernel(tc, x, mask, W_kv_words, W_kv_scales, b_kv, ou
         def multiply(t):
             engine = nc.vector if t == TILES - 1 else nc.gpsimd
             prod = prod_pool.tile([P, CHANNELS], F32)
-            for h in range(KEY_BANKS):
-                half = slice(h * BANK, (h + 1) * BANK)
-                engine.tensor_tensor(out=prod[:, half], in0=keys_of[t][:, half], in1=values_of[t][:, half], op=MULT)
+            middle = (ACC_WIDTH + CHANNELS) // 2
+            for part in (slice(0, ACC_WIDTH), slice(ACC_WIDTH, middle), slice(middle, CHANNELS)):
+                engine.tensor_tensor(out=prod[:, part], in0=keys_of[t][:, part], in1=values_of[t][:, part], op=MULT)
             prod_of[t] = prod
 
         def opens_chunk(t):
@@ -202,6 +244,9 @@ def tile_hydraattention_pa_kernel(tc, x, mask, W_kv_words, W_kv_scales, b_kv, ou
         keys_of = {}
         values_of = {}
         prod_of = {}
+        acc_of = {}
+        waiting = []
+        served = {"count": 0}
 
         for n in range(BANKS_PER_TILE):
             spread = psum.tile([P, BANK], F32, tag="acc")
@@ -235,10 +280,25 @@ def tile_hydraattention_pa_kernel(tc, x, mask, W_kv_words, W_kv_scales, b_kv, ou
                 grouped = regroup(nc.scalar.copy, (t + REGROUP_AHEAD) // CHUNK_TILES)
             if opens_chunk(t + QUANTISE_AHEAD):
                 quantise((t + QUANTISE_AHEAD) // CHUNK_TILES, grouped)
+            if t >= 1 and not pooled_directly(t - 1):
+                accumulate(t - 1)
 
+        while_left = len(waiting) - served["count"]
+        for k in range(while_left):
+            place_behind_pass(NO_TILE, 0)
+        sums_view = sums[:, 0:ROWS].rearrange("p (b strip s) -> p b strip s", b=IMAGES, s=SUMS)
+        pooled_view = pooled[:].rearrange("p (b i) strip s -> p b i strip s", b=IMAGES)
         nc.vector.tensor_reduce(
-            out=sums[:, 0:ROWS].rearrange("p (b rest) -> p b rest", b=IMAGES),
-            in_=pooled[:].rearrange("p (b i) strip s -> p b (strip s) i", b=IMAGES),
+            out=sums_view[:, :, 0:ACC_STRIPS, :].rearrange("p b strip s -> p b (strip s)"),
+            in_=pooled_view[:, :, 0 : TILES_PER_IMAGE : TILES_PER_IMAGE - 1, 0:ACC_STRIPS, :].rearrange(
+                "p b i strip s -> p b (strip s) i"
+            ),
+            axis=mybir.AxisListType.X,
+            op=ADD,
+        )
+        nc.vector.tensor_reduce(
+            out=sums_view[:, :, ACC_STRIPS:STRIPS, :].rearrange("p b strip s -> p b (strip s)"),
+            in_=pooled_view[:, :, :, ACC_STRIPS:STRIPS, :].rearrange("p b i strip s -> p b (strip s) i"),
             axis=mybir.AxisListType.X,
             op=ADD,
         )

@@ -305,5 +305,5 @@ def tile_hydraattention_pa_kernel(tc, x, mask, W_kv_words, W_kv_scales, b_kv, ou
         turned = psum.tile([P, BANK], F32, tag="acc")
         nc.tensor.transpose(out=turned[:, 0:P], in_=sums[:], identity=ident[:])
         nc.vector.tensor_copy(out=rows[:], in_=turned[:, 0:P])
-        for s, out in enumerate((out_0, out_1)):
-            nc.sync.dma_start(out=out.rearrange("b o (strip ch) -> (b o strip) ch", ch=P), in_=rows[s:ROWS:SUMS, :])
+        for s, (queue, out) in enumerate(((nc.sync, out_0), (nc.scalar, out_1))):
+            queue.dma_start(out=out.rearrange("b o (strip ch) -> (b o strip) ch", ch=P), in_=rows[s:ROWS:SUMS, :])

@@ -38,9 +38,11 @@ RUN = 4
 STRIPS = CHANNELS // P
 SUMS = 2
 ROWS = SUMS * IMAGES * STRIPS
-NO_TILE = -1
 ACC_STRIPS = 2
 ACC_WIDTH = ACC_STRIPS * P
+LATE_TILES = 2
+LATE_BASE = P
+WARM_UP = 6
 REGROUP_AHEAD = 3
 QUANTISE_AHEAD = 2
 
@@ -62,17 +64,17 @@ def tile_hydraattention_pa_kernel(tc, x, mask, W_kv_words, W_kv_scales, b_kv, ou
         psum_sums = ctx.enter_context(tc.psum_pool(name="psum_sums", bufs=1))
         ctx.enter_context(tc.manual_schedule())
 
-        raw = keep.tile([P, CHUNKS, PACK, PASSES * CHUNK], BF16)
+        raw = keep.tile([P, CHUNKS, PASSES, PACK, CHUNK], BF16)
         x_codes = keep.tile([P, CHUNKS, PASSES * CHUNK], U32, align_bytes=64)
         x_scales = keep.tile([P, CHUNKS, PASSES * CHUNK], U8, align_bytes=64)
-        w_words = keep.tile([P, PASSES, 2 * KV], U8, align_bytes=64)
+        w_words = keep.tile([P, BANKS_PER_TILE, PASSES, 2 * BANK], U8, align_bytes=64)
         w_scales = keep.tile([P, PASSES, KV], U8, align_bytes=64)
-        bias_row = keep.tile([P, KV], BF16)
-        ones = keep.tile([P, P], BF16)
+        bias_rows = keep.tile([P, BANK], BF16)
+        ident_bf16 = keep.tile([P, P], BF16)
+        warm = keep.tile([P, BANK], BF16)
         bias = keep.tile([P, KV], BF16)
         ident = keep.tile([P, P], F32)
         mask_rows = keep.tile([P, P], BF16)
-        mask_f32 = keep.tile([P, P], F32)
         mask_pair = keep.tile([P, TILES, SUMS], F32)
         sumsq = keep.tile([P, TILES], F32)
         inv_norm = keep.tile([P, TILES], F32)
@@ -84,15 +86,18 @@ def tile_hydraattention_pa_kernel(tc, x, mask, W_kv_words, W_kv_scales, b_kv, ou
         table_in = keep.tile([P, 1], F32)
         table_out = keep.tile([P, 1], F32)
         pooled = psum_sums.tile([P, TILES, STRIPS, SUMS], F32)
+        late_weights = keep.tile([P, LATE_TILES, 2 * P], F32)
 
-        nc.vector.memset(bias_row[:].bitcast(I32), 0)
-        nc.scalar.dma_start(out=bias_row[0:1, :], in_=b_kv.rearrange("(o kv) -> o kv", o=1))
-        nc.vector.memset(w_scales[:].rearrange("p g kv -> p (g kv)").bitcast(I32), 0)
-        nc.vector.memset(ones[:], 1.0)
+        nc.vector.memset(bias_rows[:].bitcast(I32), 0)
+        nc.scalar.dma_start(out=bias_rows[0:BANKS_PER_TILE, :], in_=b_kv.rearrange("(n c) -> n c", c=BANK))
+        nc.vector.memset(warm[:].bitcast(I32), 0)
+        nc.vector.memset(mask_rows[:].bitcast(I32), 0)
+        make_identity(nc, ident_bf16[:])
         nc.vector.memset(table_in[:], 1.0)
+        nc.vector.memset(w_scales[:].rearrange("p g kv -> p (g kv)").bitcast(I32), 0)
         nc.scalar.activation(out=table_out[:], in_=table_in[:], func=ACT.Abs_reciprocal_sqrt)
-        nc.gpsimd.memset(mask_rows[:], 0.0)
         nc.gpsimd.memset(sums[:], 0.0)
+        nc.gpsimd.memset(late_weights[:], 0.0)
         nc.gpsimd.memset(zeros[:], 0.0)
         nc.gpsimd.memset(one_col[:], 1.0)
         make_identity(nc, ident[:])
@@ -103,45 +108,50 @@ def tile_hydraattention_pa_kernel(tc, x, mask, W_kv_words, W_kv_scales, b_kv, ou
             b, quarter = divmod(chunk, CHUNKS_PER_IMAGE)
             for g in range(PASSES):
                 nc.sync.dma_start(
-                    out=raw[:, chunk, :, g * CHUNK : (g + 1) * CHUNK],
+                    out=raw[:, chunk, g],
                     in_=x_rows[b, g, :, :, quarter * CHUNK : (quarter + 1) * CHUNK],
                 )
 
-        def load_words(first_byte, last_byte):
+        def load_words(n):
             nc.sync.dma_start(
-                out=w_words[:, :, first_byte:last_byte].bitcast(I32),
-                in_=W_kv_words.rearrange("g p byte -> p g byte")[:, :, first_byte:last_byte].bitcast(I32),
+                out=w_words[:, n].bitcast(I32),
+                in_=W_kv_words.rearrange("g p byte -> p g byte")[:, :, 2 * n * BANK : 2 * (n + 1) * BANK].bitcast(I32),
             )
 
         load_chunk(0)
-        load_words(0, KV)
+        load_words(0)
         for r in range(PACK):
             nc.sync.dma_start(
                 out=w_scales[r:P:QUADRANT, :, :].bitcast(I32),
                 in_=W_kv_scales[:, r:SCALE_ROWS:PACK, :].rearrange("g q kv -> q g kv").bitcast(I32),
             )
-        load_words(KV, 2 * KV)
-        load_chunk(1)
+        load_words(1)
         nc.sync.dma_start(
             out=mask_rows[0:TILES, :],
             in_=mask.rearrange("b o (i row) col -> (b o i) (row col)", i=TILES_PER_IMAGE),
         )
+        for n in range(KEY_BANKS, BANKS_PER_TILE):
+            load_words(n)
+        load_chunk(1)
         for chunk in range(2, CHUNKS):
             load_chunk(chunk)
 
-        def regroup(copy, chunk):
-            grouped = stage.tile([P, PASSES * CHUNK, PACK], BF16, align_bytes=64)
-            copy(
-                out=grouped[:].rearrange("p (run e) j -> p run j e", e=RUN),
-                in_=raw[:, chunk].rearrange("p j (run e) -> p run j e", e=RUN),
-            )
+        def new_grouped():
+            grouped = stage.tile([P, PASSES, CHUNK, PACK], BF16, align_bytes=64)
             return grouped
 
-        def quantise(chunk, grouped):
+        def regroup(copy, chunk, grouped, g):
+            copy(
+                out=grouped[:, g].rearrange("p (run e) j -> p run j e", e=RUN),
+                in_=raw[:, chunk, g].rearrange("p j (run e) -> p run j e", e=RUN),
+            )
+
+        def quantise(chunk, grouped, first, last):
+            columns = slice(first * CHUNK, (last + 1) * CHUNK)
             nc.vector.quantize_mx(
-                out=x_codes[:, chunk, :].bitcast(FP8X4),
-                scales=x_scales[:, chunk, :],
-                in_=grouped[:].rearrange("p px j -> p (px j)"),
+                out=x_codes[:, chunk, columns].bitcast(FP8X4),
+                scales=x_scales[:, chunk, columns],
+                in_=grouped[:, first : last + 1].rearrange("p g px j -> p (g px j)"),
             )
 
         def pool_strip(t, strip):
@@ -153,8 +163,14 @@ def tile_hydraattention_pa_kernel(tc, x, mask, W_kv_words, W_kv_scales, b_kv, ou
                 stop=True,
             )
 
+        def is_late(t):
+            return t >= TILES - LATE_TILES
+
         def pooled_directly(t):
-            return t % TILES_PER_IMAGE == TILES_PER_IMAGE - 1
+            return t % TILES_PER_IMAGE == TILES_PER_IMAGE - 1 and not is_late(t)
+
+        def accumulates(t):
+            return not is_late(t) and not pooled_directly(t)
 
         def pool_running_sum(b, strip, s):
             nc.tensor.matmul(
@@ -165,12 +181,17 @@ def tile_hydraattention_pa_kernel(tc, x, mask, W_kv_words, W_kv_scales, b_kv, ou
                 stop=True,
             )
 
-        def place_behind_pass(pool_tile, strip):
-            if pool_tile != NO_TILE and (strip >= ACC_STRIPS or pooled_directly(pool_tile)):
-                pool_strip(pool_tile, strip)
-            elif served["count"] < len(waiting):
-                pool_running_sum(*waiting[served["count"]])
-                served["count"] += 1
+        def jobs_behind_passes(pool_tile):
+            strips = [lambda strip=strip: pool_strip(pool_tile, strip) for strip in range(ACC_STRIPS, STRIPS)]
+            if pooled_directly(pool_tile):
+                return strips + [lambda strip=strip: pool_strip(pool_tile, strip) for strip in range(ACC_STRIPS)]
+            if is_late(pool_tile + 1):
+                return strips + [lambda job=job: pool_running_sum(*job) for job in waiting]
+            jobs = []
+            for place in range(ACC_STRIPS):
+                job = waiting.pop(0) if waiting else None
+                jobs.append(lambda job=job: pool_running_sum(*job) if job else None)
+            return jobs + strips
 
         def accumulate(t):
             b, i = divmod(t, TILES_PER_IMAGE)
@@ -186,27 +207,25 @@ def tile_hydraattention_pa_kernel(tc, x, mask, W_kv_words, W_kv_scales, b_kv, ou
                     op1=ADD,
                 )
             acc_of[b] = acc
-            if pooled_directly(t + 1):
+            if not accumulates(t + 1):
                 waiting.extend((b, strip, s) for strip in range(ACC_STRIPS) for s in range(SUMS))
 
-        def project_bank(t, n, pool_tile):
+        def project_bank(t, n, jobs):
             chunk, place = divmod(t, CHUNK_TILES)
-            acc = None
-            if t < TILES:
-                acc = psum.tile([P, BANK], F32, tag="acc")
+            acc = psum.tile([P, BANK], F32, tag="acc")
             for g in range(PASSES):
-                if t < TILES:
-                    pixels = slice(g * CHUNK + place * P, g * CHUNK + (place + 1) * P)
-                    nc.tensor.matmul_mx(
-                        out=acc[:],
-                        lhsT=x_codes[:, chunk, pixels].bitcast(FP8X4),
-                        lhsT_scale=x_scales[:, chunk, pixels],
-                        rhs=w_words[:, g, 2 * n * BANK : 2 * (n + 1) * BANK].bitcast(FP4X4),
-                        rhs_scale=w_scales[:, g, n * BANK : (n + 1) * BANK],
-                        start=(g == 0),
-                        stop=(g == PASSES - 1),
-                    )
-                place_behind_pass(pool_tile, n * PASSES + g)
+                pixels = slice(g * CHUNK + place * P, g * CHUNK + (place + 1) * P)
+                nc.tensor.matmul_mx(
+                    out=acc[:],
+                    lhsT=x_codes[:, chunk, pixels].bitcast(FP8X4),
+                    lhsT_scale=x_scales[:, chunk, pixels],
+                    rhs=w_words[:, n, g].bitcast(FP4X4),
+                    rhs_scale=w_scales[:, g, n * BANK : (n + 1) * BANK],
+                    start=(g == 0),
+                    stop=(g == PASSES - 1),
+                )
+                if jobs:
+                    jobs.pop(0)()
             return acc
 
         def new_biased():
@@ -226,15 +245,18 @@ def tile_hydraattention_pa_kernel(tc, x, mask, W_kv_words, W_kv_scales, b_kv, ou
             squares = scratch.tile([P, CHANNELS], F32)
             nc.scalar.activation(out=squares[:], in_=keys_of[t][:], func=ACT.Square, accum_out=sumsq[:, t : t + 1])
             nc.scalar.activation(out=inv_norm[:, t : t + 1], in_=sumsq[:, t : t + 1], func=ACT.Abs_reciprocal_sqrt)
-            nc.scalar.activation(
-                out=weights[:, t, :], in_=mask_pair[:, t, :], func=ACT.Copy, scale=inv_norm[:, t : t + 1]
-            )
+            pair = weights[:, t, :]
+            if is_late(t):
+                pair = late_weights[:, t - (TILES - LATE_TILES), LATE_BASE : LATE_BASE + SUMS]
+            nc.scalar.activation(out=pair, in_=mask_pair[:, t, :], func=ACT.Copy, scale=inv_norm[:, t : t + 1])
 
         def multiply(t):
-            engine = nc.vector if t == TILES - 1 else nc.gpsimd
+            last = t == TILES - 1
+            engine = nc.vector if last else nc.gpsimd
             prod = prod_pool.tile([P, CHANNELS], F32)
             middle = (ACC_WIDTH + CHANNELS) // 2
-            for part in (slice(0, ACC_WIDTH), slice(ACC_WIDTH, middle), slice(middle, CHANNELS)):
+            parts = [slice(ACC_WIDTH, middle), slice(middle, CHANNELS), slice(0, ACC_WIDTH)]
+            for part in parts:
                 engine.tensor_tensor(out=prod[:, part], in0=keys_of[t][:, part], in1=values_of[t][:, part], op=MULT)
             prod_of[t] = prod
 
@@ -246,64 +268,92 @@ def tile_hydraattention_pa_kernel(tc, x, mask, W_kv_words, W_kv_scales, b_kv, ou
         prod_of = {}
         acc_of = {}
         waiting = []
-        served = {"count": 0}
 
-        for n in range(BANKS_PER_TILE):
+        def spread_bias(n):
             spread = psum.tile([P, BANK], F32, tag="acc")
             nc.tensor.matmul(
-                out=spread[:], lhsT=ones[:], rhs=bias_row[:, n * BANK : (n + 1) * BANK], start=True, stop=True
+                out=spread[:],
+                lhsT=ident_bf16[:, n : n + 1].to_broadcast([P, P]),
+                rhs=bias_rows[:],
+                start=True,
+                stop=True,
             )
             nc.scalar.copy(out=bias[:, n * BANK : (n + 1) * BANK], in_=spread[:])
-        quantise(0, regroup(nc.vector.tensor_copy, 0))
-        grouped = regroup(nc.scalar.copy, 1)
-        banks = [project_bank(0, n, NO_TILE) for n in range(BANKS_PER_TILE)]
 
-        nc.scalar.copy(out=mask_f32[:], in_=mask_rows[:])
-        mask_cols = psum.tile([P, BANK], F32, tag="acc")
-        nc.tensor.transpose(out=mask_cols[:, 0:P], in_=mask_f32[:], identity=ident[:])
+        first_grouped = new_grouped()
+        for g in range(PASSES):
+            regroup(nc.vector.tensor_copy, 0, first_grouped, g)
+        for g in range(PASSES):
+            quantise(0, first_grouped, g, g)
+        idle = psum.tile([P, BANK], F32, tag="acc")
+        for n in range(WARM_UP):
+            nc.tensor.matmul(out=idle[:], lhsT=warm[:, 0:P], rhs=warm[:], start=True, stop=True)
+        for n in range(BANKS_PER_TILE - 1):
+            spread_bias(n)
+        banks = [project_bank(0, 0, [])]
+        spread_bias(BANKS_PER_TILE - 1)
+        banks += [project_bank(0, n, []) for n in range(1, BANKS_PER_TILE)]
+        mask_cols = psum.tile([P, P], BF16, tag="acc")
+        nc.tensor.transpose(out=mask_cols[:], in_=mask_rows[:], identity=ident_bf16[:])
         nc.scalar.activation(out=mask_pair[:, :, 0], in_=mask_cols[:, 0:TILES], func=ACT.Copy, scale=-1.0, bias=1.0)
         nc.scalar.copy(out=mask_pair[:, :, 1], in_=mask_cols[:, 0:TILES])
+        grouped = new_grouped()
+        regroup(nc.scalar.copy, 1, grouped, 0)
 
-        for t in range(TILES + 1):
-            if t < TILES:
-                keys_of[t] = new_biased()
-                for n in range(KEY_BANKS):
-                    add_bias(keys_of[t], banks, n)
-                weigh(t)
-                values_of[t] = new_biased()
-                for n in range(KEY_BANKS, BANKS_PER_TILE):
-                    add_bias(values_of[t], banks, n)
-                multiply(t)
-            pool_tile = t - 1 if t >= 1 else NO_TILE
-            banks = [project_bank(t + 1, n, pool_tile) for n in range(BANKS_PER_TILE)]
-            if opens_chunk(t + REGROUP_AHEAD):
-                grouped = regroup(nc.scalar.copy, (t + REGROUP_AHEAD) // CHUNK_TILES)
+        for t in range(TILES):
+            keys_of[t] = new_biased()
+            for n in range(KEY_BANKS):
+                add_bias(keys_of[t], banks, n)
+            weigh(t)
+            values_of[t] = new_biased()
+            for n in range(KEY_BANKS, BANKS_PER_TILE):
+                add_bias(values_of[t], banks, n)
+            multiply(t)
+            if t == 0:
+                regroup(nc.vector.tensor_copy, 1, grouped, 1)
             if opens_chunk(t + QUANTISE_AHEAD):
-                quantise((t + QUANTISE_AHEAD) // CHUNK_TILES, grouped)
-            if t >= 1 and not pooled_directly(t - 1):
+                quantise((t + QUANTISE_AHEAD) // CHUNK_TILES, grouped, 0, PASSES - 1)
+            jobs = jobs_behind_passes(t - 1) if t >= 1 and not is_late(t) else []
+            if t >= 1 and accumulates(t - 1):
                 accumulate(t - 1)
+            if t + 1 < TILES:
+                if is_late(t):
+                    jobs = jobs_behind_passes(t - 1)
+                banks = [project_bank(t + 1, n, jobs) for n in range(BANKS_PER_TILE)]
+                for job in jobs:
+                    job()
+            if opens_chunk(t + REGROUP_AHEAD):
+                grouped = new_grouped()
+                for g in range(PASSES):
+                    regroup(nc.scalar.copy, (t + REGROUP_AHEAD) // CHUNK_TILES, grouped, g)
 
-        while_left = len(waiting) - served["count"]
-        for k in range(while_left):
-            place_behind_pass(NO_TILE, 0)
         sums_view = sums[:, 0:ROWS].rearrange("p (b strip s) -> p b strip s", b=IMAGES, s=SUMS)
-        pooled_view = pooled[:].rearrange("p (b i) strip s -> p b i strip s", b=IMAGES)
-        nc.vector.tensor_reduce(
-            out=sums_view[:, :, 0:ACC_STRIPS, :].rearrange("p b strip s -> p b (strip s)"),
-            in_=pooled_view[:, :, 0 : TILES_PER_IMAGE : TILES_PER_IMAGE - 1, 0:ACC_STRIPS, :].rearrange(
-                "p b i strip s -> p b (strip s) i"
-            ),
-            axis=mybir.AxisListType.X,
-            op=ADD,
-        )
-        nc.vector.tensor_reduce(
-            out=sums_view[:, :, ACC_STRIPS:STRIPS, :].rearrange("p b strip s -> p b (strip s)"),
-            in_=pooled_view[:, :, :, ACC_STRIPS:STRIPS, :].rearrange("p b i strip s -> p b (strip s) i"),
-            axis=mybir.AxisListType.X,
-            op=ADD,
-        )
+        for b in range(IMAGES):
+            tiles = [t for t in range(b * TILES_PER_IMAGE, (b + 1) * TILES_PER_IMAGE) if not is_late(t)]
+            acc_tiles = [tiles[0]] + [t for t in tiles if pooled_directly(t)]
+            for part, strips in ((tiles, slice(ACC_STRIPS, STRIPS)), (acc_tiles, slice(0, ACC_STRIPS))):
+                step = part[-1] - part[0] if len(part) == 2 else 1
+                nc.vector.tensor_reduce(
+                    out=sums_view[:, b, strips, :].rearrange("p strip s -> p (strip s)"),
+                    in_=pooled[:, part[0] : part[-1] + 1 : step, strips, :].rearrange("p i strip s -> p (strip s) i"),
+                    axis=mybir.AxisListType.X,
+                    op=ADD,
+                )
+
         turned = psum.tile([P, BANK], F32, tag="acc")
-        nc.tensor.transpose(out=turned[:, 0:P], in_=sums[:], identity=ident[:])
+        strip_order = [*range(ACC_STRIPS, STRIPS), *range(ACC_STRIPS)]
+        terms = []
+        for t in range(TILES - LATE_TILES, TILES):
+            for strip in strip_order:
+                row = SUMS * (STRIPS * (t // TILES_PER_IMAGE) + strip)
+                window = slice(LATE_BASE - row, LATE_BASE - row + P)
+                products = prod_of[t][:, strip * P : (strip + 1) * P]
+                terms.append((late_weights[:, t - (TILES - LATE_TILES), window], products))
+        terms.insert(len(terms) - STRIPS // 2, (sums[:], ident[:]))
+        for i, (stationary, moving) in enumerate(terms):
+            nc.tensor.matmul(
+                out=turned[:, 0:P], lhsT=stationary, rhs=moving, start=(i == 0), stop=(i == len(terms) - 1)
+            )
         nc.vector.tensor_copy(out=rows[:], in_=turned[:, 0:P])
         for s, (queue, out) in enumerate(((nc.sync, out_0), (nc.scalar, out_1))):
             queue.dma_start(out=out.rearrange("b o (strip ch) -> (b o strip) ch", ch=P), in_=rows[s:ROWS:SUMS, :])

@@ -87,6 +87,7 @@ def tile_hydraattention_pa_kernel(tc, x, mask, W_kv_words, W_kv_scales, b_kv, ou
         table_out = keep.tile([P, 1], F32)
         pooled = psum_sums.tile([P, TILES, STRIPS, SUMS], F32)
         late_weights = keep.tile([P, LATE_TILES, 2 * P], F32)
+        one_hot = keep.tile([P, 2 * P], F32)
 
         nc.vector.memset(bias_rows[:].bitcast(I32), 0)
         nc.scalar.dma_start(out=bias_rows[0:BANKS_PER_TILE, :], in_=b_kv.rearrange("(n c) -> n c", c=BANK))
@@ -98,6 +99,8 @@ def tile_hydraattention_pa_kernel(tc, x, mask, W_kv_words, W_kv_scales, b_kv, ou
         nc.scalar.activation(out=table_out[:], in_=table_in[:], func=ACT.Abs_reciprocal_sqrt)
         nc.gpsimd.memset(sums[:], 0.0)
         nc.gpsimd.memset(late_weights[:], 0.0)
+        nc.gpsimd.memset(one_hot[:], 0.0)
+        nc.gpsimd.memset(one_hot[:, LATE_BASE : LATE_BASE + 1], 1.0)
         nc.gpsimd.memset(zeros[:], 0.0)
         nc.gpsimd.memset(one_col[:], 1.0)
         make_identity(nc, ident[:])
@@ -158,19 +161,13 @@ def tile_hydraattention_pa_kernel(tc, x, mask, W_kv_words, W_kv_scales, b_kv, ou
             nc.tensor.matmul(
                 out=pooled[:, t, strip, :],
                 lhsT=prod_of[t][:, strip * P : (strip + 1) * P],
-                rhs=weights[:, t, :],
+                rhs=weight_pair(t),
                 start=True,
                 stop=True,
             )
 
         def is_late(t):
             return t >= TILES - LATE_TILES
-
-        def pooled_directly(t):
-            return t % TILES_PER_IMAGE == TILES_PER_IMAGE - 1 and not is_late(t)
-
-        def accumulates(t):
-            return not is_late(t) and not pooled_directly(t)
 
         def pool_running_sum(b, strip, s):
             nc.tensor.matmul(
@@ -182,16 +179,11 @@ def tile_hydraattention_pa_kernel(tc, x, mask, W_kv_words, W_kv_scales, b_kv, ou
             )
 
         def jobs_behind_passes(pool_tile):
-            strips = [lambda strip=strip: pool_strip(pool_tile, strip) for strip in range(ACC_STRIPS, STRIPS)]
-            if pooled_directly(pool_tile):
-                return strips + [lambda strip=strip: pool_strip(pool_tile, strip) for strip in range(ACC_STRIPS)]
-            if is_late(pool_tile + 1):
-                return strips + [lambda job=job: pool_running_sum(*job) for job in waiting]
             jobs = []
             for place in range(ACC_STRIPS):
                 job = waiting.pop(0) if waiting else None
                 jobs.append(lambda job=job: pool_running_sum(*job) if job else None)
-            return jobs + strips
+            return jobs + [lambda strip=strip: pool_strip(pool_tile, strip) for strip in range(ACC_STRIPS, STRIPS)]
 
         def accumulate(t):
             b, i = divmod(t, TILES_PER_IMAGE)
@@ -201,13 +193,13 @@ def tile_hydraattention_pa_kernel(tc, x, mask, W_kv_words, W_kv_scales, b_kv, ou
                 nc.vector.scalar_tensor_tensor(
                     out=acc[:, s, :],
                     in0=prod_of[t][:, 0:ACC_WIDTH],
-                    scalar=weights[:, t, s : s + 1],
+                    scalar=weight_pair(t)[:, s : s + 1],
                     in1=before[:, s, :],
                     op0=MULT,
                     op1=ADD,
                 )
             acc_of[b] = acc
-            if not accumulates(t + 1):
+            if t == TILES_PER_IMAGE - 1:
                 waiting.extend((b, strip, s) for strip in range(ACC_STRIPS) for s in range(SUMS))
 
         def project_bank(t, n, jobs):
@@ -241,14 +233,16 @@ def tile_hydraattention_pa_kernel(tc, x, mask, W_kv_words, W_kv_scales, b_kv, ou
                 op=ADD,
             )
 
+        def weight_pair(t):
+            if is_late(t):
+                return late_weights[:, t - (TILES - LATE_TILES), LATE_BASE : LATE_BASE + SUMS]
+            return weights[:, t, :]
+
         def weigh(t):
             squares = scratch.tile([P, CHANNELS], F32)
             nc.scalar.activation(out=squares[:], in_=keys_of[t][:], func=ACT.Square, accum_out=sumsq[:, t : t + 1])
             nc.scalar.activation(out=inv_norm[:, t : t + 1], in_=sumsq[:, t : t + 1], func=ACT.Abs_reciprocal_sqrt)
-            pair = weights[:, t, :]
-            if is_late(t):
-                pair = late_weights[:, t - (TILES - LATE_TILES), LATE_BASE : LATE_BASE + SUMS]
-            nc.scalar.activation(out=pair, in_=mask_pair[:, t, :], func=ACT.Copy, scale=inv_norm[:, t : t + 1])
+            nc.scalar.activation(out=weight_pair(t), in_=mask_pair[:, t, :], func=ACT.Copy, scale=inv_norm[:, t : t + 1])
 
         def multiply(t):
             last = t == TILES - 1
@@ -313,43 +307,46 @@ def tile_hydraattention_pa_kernel(tc, x, mask, W_kv_words, W_kv_scales, b_kv, ou
                 regroup(nc.vector.tensor_copy, 1, grouped, 1)
             if opens_chunk(t + QUANTISE_AHEAD):
                 quantise((t + QUANTISE_AHEAD) // CHUNK_TILES, grouped, 0, PASSES - 1)
-            jobs = jobs_behind_passes(t - 1) if t >= 1 and not is_late(t) else []
-            if t >= 1 and accumulates(t - 1):
-                accumulate(t - 1)
             if t + 1 < TILES:
-                if is_late(t):
-                    jobs = jobs_behind_passes(t - 1)
+                jobs = jobs_behind_passes(t - 1) if t >= 1 else []
                 banks = [project_bank(t + 1, n, jobs) for n in range(BANKS_PER_TILE)]
-                for job in jobs:
-                    job()
+            if t >= 1:
+                accumulate(t - 1)
             if opens_chunk(t + REGROUP_AHEAD):
                 grouped = new_grouped()
                 for g in range(PASSES):
                     regroup(nc.scalar.copy, (t + REGROUP_AHEAD) // CHUNK_TILES, grouped, g)
 
+        accumulate(TILES - 1)
+
         sums_view = sums[:, 0:ROWS].rearrange("p (b strip s) -> p b strip s", b=IMAGES, s=SUMS)
         for b in range(IMAGES):
-            tiles = [t for t in range(b * TILES_PER_IMAGE, (b + 1) * TILES_PER_IMAGE) if not is_late(t)]
-            acc_tiles = [tiles[0]] + [t for t in tiles if pooled_directly(t)]
-            for part, strips in ((tiles, slice(ACC_STRIPS, STRIPS)), (acc_tiles, slice(0, ACC_STRIPS))):
-                step = part[-1] - part[0] if len(part) == 2 else 1
-                nc.vector.tensor_reduce(
-                    out=sums_view[:, b, strips, :].rearrange("p strip s -> p (strip s)"),
-                    in_=pooled[:, part[0] : part[-1] + 1 : step, strips, :].rearrange("p i strip s -> p (strip s) i"),
-                    axis=mybir.AxisListType.X,
-                    op=ADD,
-                )
+            first = b * TILES_PER_IMAGE
+            end = min(first + TILES_PER_IMAGE, TILES - LATE_TILES)
+            nc.vector.tensor_reduce(
+                out=sums_view[:, b, ACC_STRIPS:STRIPS, :].rearrange("p strip s -> p (strip s)"),
+                in_=pooled[:, first:end, ACC_STRIPS:STRIPS, :].rearrange("p i strip s -> p (strip s) i"),
+                axis=mybir.AxisListType.X,
+                op=ADD,
+            )
+        nc.vector.tensor_copy(out=sums_view[:, 0, 0:ACC_STRIPS, :], in_=pooled[:, 0, 0:ACC_STRIPS, :])
 
         turned = psum.tile([P, BANK], F32, tag="acc")
-        strip_order = [*range(ACC_STRIPS, STRIPS), *range(ACC_STRIPS)]
+
+        def window(strip, s):
+            start = LATE_BASE - (SUMS * (STRIPS * (IMAGES - 1) + strip) + s)
+            return slice(start, start + P)
+
         terms = []
         for t in range(TILES - LATE_TILES, TILES):
-            for strip in strip_order:
-                row = SUMS * (STRIPS * (t // TILES_PER_IMAGE) + strip)
-                window = slice(LATE_BASE - row, LATE_BASE - row + P)
+            for strip in range(ACC_STRIPS, STRIPS):
                 products = prod_of[t][:, strip * P : (strip + 1) * P]
-                terms.append((late_weights[:, t - (TILES - LATE_TILES), window], products))
-        terms.insert(len(terms) - STRIPS // 2, (sums[:], ident[:]))
+                terms.append((late_weights[:, t - (TILES - LATE_TILES), window(strip, 0)], products))
+        for strip in range(ACC_STRIPS):
+            for s in range(SUMS):
+                running = acc_of[IMAGES - 1][:, s, strip * P : (strip + 1) * P]
+                terms.append((one_hot[:, window(strip, s)], running))
+        terms.append((sums[:], ident[:]))
         for i, (stationary, moving) in enumerate(terms):
             nc.tensor.matmul(
                 out=turned[:, 0:P], lhsT=stationary, rhs=moving, start=(i == 0), stop=(i == len(terms) - 1)

@@ -40,10 +40,12 @@ SUMS = 2
 ROWS = SUMS * IMAGES * STRIPS
 ACC_STRIPS = 2
 ACC_WIDTH = ACC_STRIPS * P
+ACC_FIRST = STRIPS - ACC_STRIPS
+ACC_START = ACC_FIRST * P
 LATE_TILES = 2
 LATE_BASE = P
 WARM_UP = 6
-REGROUP_AHEAD = 3
+REGROUP_AHEAD = 4
 QUANTISE_AHEAD = 2
 
 assert STRIPS == BANKS_PER_TILE * PASSES
@@ -55,10 +57,10 @@ def tile_hydraattention_pa_kernel(tc, x, mask, W_kv_words, W_kv_scales, b_kv, ou
     nc = tc.nc
     with ExitStack() as ctx:
         keep = ctx.enter_context(tc.tile_pool(name="keep", bufs=1))
-        stage = ctx.enter_context(tc.tile_pool(name="stage", bufs=2))
+        stage = ctx.enter_context(tc.tile_pool(name="stage", bufs=3))
         biased_pool = ctx.enter_context(tc.tile_pool(name="biased", bufs=6))
         scratch = ctx.enter_context(tc.tile_pool(name="scratch", bufs=2))
-        prod_pool = ctx.enter_context(tc.tile_pool(name="prod", bufs=3))
+        prod_pool = ctx.enter_context(tc.tile_pool(name="prod", bufs=4))
         acc_pool = ctx.enter_context(tc.tile_pool(name="acc", bufs=4))
         psum = ctx.enter_context(tc.psum_pool(name="psum", bufs=7))
         psum_sums = ctx.enter_context(tc.psum_pool(name="psum_sums", bufs=1))
@@ -169,10 +171,14 @@ def tile_hydraattention_pa_kernel(tc, x, mask, W_kv_words, W_kv_scales, b_kv, ou
         def is_late(t):
             return t >= TILES - LATE_TILES
 
+        def running_sum(b, strip, s):
+            first = (strip - ACC_FIRST) * P
+            return acc_of[b][:, s, first : first + P]
+
         def pool_running_sum(b, strip, s):
             nc.tensor.matmul(
                 out=pooled[:, b * TILES_PER_IMAGE, strip, s : s + 1],
-                lhsT=acc_of[b][:, s, strip * P : (strip + 1) * P],
+                lhsT=running_sum(b, strip, s),
                 rhs=one_col[:],
                 start=True,
                 stop=True,
@@ -183,7 +189,7 @@ def tile_hydraattention_pa_kernel(tc, x, mask, W_kv_words, W_kv_scales, b_kv, ou
             for place in range(ACC_STRIPS):
                 job = waiting.pop(0) if waiting else None
                 jobs.append(lambda job=job: pool_running_sum(*job) if job else None)
-            return jobs + [lambda strip=strip: pool_strip(pool_tile, strip) for strip in range(ACC_STRIPS, STRIPS)]
+            return jobs + [lambda strip=strip: pool_strip(pool_tile, strip) for strip in product_order(pool_tile)]
 
         def accumulate(t):
             b, i = divmod(t, TILES_PER_IMAGE)
@@ -192,7 +198,7 @@ def tile_hydraattention_pa_kernel(tc, x, mask, W_kv_words, W_kv_scales, b_kv, ou
             for s in range(SUMS):
                 nc.vector.scalar_tensor_tensor(
                     out=acc[:, s, :],
-                    in0=prod_of[t][:, 0:ACC_WIDTH],
+                    in0=prod_of[t][:, ACC_START:CHANNELS],
                     scalar=weight_pair(t)[:, s : s + 1],
                     in1=before[:, s, :],
                     op0=MULT,
@@ -200,7 +206,7 @@ def tile_hydraattention_pa_kernel(tc, x, mask, W_kv_words, W_kv_scales, b_kv, ou
                 )
             acc_of[b] = acc
             if t == TILES_PER_IMAGE - 1:
-                waiting.extend((b, strip, s) for strip in range(ACC_STRIPS) for s in range(SUMS))
+                waiting.extend((b, strip, s) for strip in range(ACC_FIRST, STRIPS) for s in range(SUMS))
 
         def project_bank(t, n, jobs):
             chunk, place = divmod(t, CHUNK_TILES)
@@ -244,15 +250,22 @@ def tile_hydraattention_pa_kernel(tc, x, mask, W_kv_words, W_kv_scales, b_kv, ou
             nc.scalar.activation(out=inv_norm[:, t : t + 1], in_=sumsq[:, t : t + 1], func=ACT.Abs_reciprocal_sqrt)
             nc.scalar.activation(out=weight_pair(t), in_=mask_pair[:, t, :], func=ACT.Copy, scale=inv_norm[:, t : t + 1])
 
-        def multiply(t):
-            last = t == TILES - 1
-            engine = nc.vector if last else nc.gpsimd
+        middle = ACC_START // 2
+
+        def product_order(t):
+            strips = list(range(ACC_FIRST))
+            half = middle // P
+            return strips if t == TILES - 1 else strips[half:] + strips[:half]
+
+        def new_product(t):
             prod = prod_pool.tile([P, CHANNELS], F32)
-            middle = (ACC_WIDTH + CHANNELS) // 2
-            parts = [slice(ACC_WIDTH, middle), slice(middle, CHANNELS), slice(0, ACC_WIDTH)]
-            for part in parts:
-                engine.tensor_tensor(out=prod[:, part], in0=keys_of[t][:, part], in1=values_of[t][:, part], op=MULT)
             prod_of[t] = prod
+
+        def multiply(engine, t, first, last):
+            part = slice(first, last)
+            engine.tensor_tensor(
+                out=prod_of[t][:, part], in0=keys_of[t][:, part], in1=values_of[t][:, part], op=MULT
+            )
 
         def opens_chunk(t):
             return t < TILES and t % CHUNK_TILES == 0
@@ -291,8 +304,8 @@ def tile_hydraattention_pa_kernel(tc, x, mask, W_kv_words, W_kv_scales, b_kv, ou
         nc.tensor.transpose(out=mask_cols[:], in_=mask_rows[:], identity=ident_bf16[:])
         nc.scalar.activation(out=mask_pair[:, :, 0], in_=mask_cols[:, 0:TILES], func=ACT.Copy, scale=-1.0, bias=1.0)
         nc.scalar.copy(out=mask_pair[:, :, 1], in_=mask_cols[:, 0:TILES])
-        grouped = new_grouped()
-        regroup(nc.scalar.copy, 1, grouped, 0)
+        grouped_of = {1: new_grouped()}
+        regroup(nc.scalar.copy, 1, grouped_of[1], 0)
 
         for t in range(TILES):
             keys_of[t] = new_biased()
@@ -300,23 +313,35 @@ def tile_hydraattention_pa_kernel(tc, x, mask, W_kv_words, W_kv_scales, b_kv, ou
                 add_bias(keys_of[t], banks, n)
             weigh(t)
             values_of[t] = new_biased()
-            for n in range(KEY_BANKS, BANKS_PER_TILE):
-                add_bias(values_of[t], banks, n)
-            multiply(t)
+            add_bias(values_of[t], banks, KEY_BANKS)
+            jobs = jobs_behind_passes(t - 1) if t >= 1 else []
+            if t >= 2:
+                accumulate(t - 2)
+            if t > 0 and opens_chunk(t + QUANTISE_AHEAD):
+                chunk = (t + QUANTISE_AHEAD) // CHUNK_TILES
+                quantise(chunk, grouped_of[chunk], 0, PASSES - 1)
+            new_product(t)
+            if t == TILES - 1:
+                multiply(nc.vector, t, 0, middle)
+            add_bias(values_of[t], banks, KEY_BANKS + 1)
+            if t == TILES - 1:
+                multiply(nc.gpsimd, t, ACC_START, CHANNELS)
+                multiply(nc.vector, t, middle, ACC_START)
+            else:
+                multiply(nc.gpsimd, t, middle, CHANNELS)
+                multiply(nc.gpsimd, t, 0, middle)
             if t == 0:
-                regroup(nc.vector.tensor_copy, 1, grouped, 1)
-            if opens_chunk(t + QUANTISE_AHEAD):
-                quantise((t + QUANTISE_AHEAD) // CHUNK_TILES, grouped, 0, PASSES - 1)
+                regroup(nc.vector.tensor_copy, 1, grouped_of[1], 1)
+                quantise(1, grouped_of[1], 0, PASSES - 1)
             if t + 1 < TILES:
-                jobs = jobs_behind_passes(t - 1) if t >= 1 else []
                 banks = [project_bank(t + 1, n, jobs) for n in range(BANKS_PER_TILE)]
-            if t >= 1:
-                accumulate(t - 1)
             if opens_chunk(t + REGROUP_AHEAD):
-                grouped = new_grouped()
+                chunk = (t + REGROUP_AHEAD) // CHUNK_TILES
+                grouped_of[chunk] = new_grouped()
                 for g in range(PASSES):
-                    regroup(nc.scalar.copy, (t + REGROUP_AHEAD) // CHUNK_TILES, grouped, g)
+                    regroup(nc.scalar.copy, chunk, grouped_of[chunk], g)
 
+        accumulate(TILES - 2)
         accumulate(TILES - 1)
 
         sums_view = sums[:, 0:ROWS].rearrange("p (b strip s) -> p b strip s", b=IMAGES, s=SUMS)
@@ -324,12 +349,12 @@ def tile_hydraattention_pa_kernel(tc, x, mask, W_kv_words, W_kv_scales, b_kv, ou
             first = b * TILES_PER_IMAGE
             end = min(first + TILES_PER_IMAGE, TILES - LATE_TILES)
             nc.vector.tensor_reduce(
-                out=sums_view[:, b, ACC_STRIPS:STRIPS, :].rearrange("p strip s -> p (strip s)"),
-                in_=pooled[:, first:end, ACC_STRIPS:STRIPS, :].rearrange("p i strip s -> p (strip s) i"),
+                out=sums_view[:, b, 0:ACC_FIRST, :].rearrange("p strip s -> p (strip s)"),
+                in_=pooled[:, first:end, 0:ACC_FIRST, :].rearrange("p i strip s -> p (strip s) i"),
                 axis=mybir.AxisListType.X,
                 op=ADD,
             )
-        nc.vector.tensor_copy(out=sums_view[:, 0, 0:ACC_STRIPS, :], in_=pooled[:, 0, 0:ACC_STRIPS, :])
+        nc.vector.tensor_copy(out=sums_view[:, 0, ACC_FIRST:STRIPS, :], in_=pooled[:, 0, ACC_FIRST:STRIPS, :])
 
         turned = psum.tile([P, BANK], F32, tag="acc")
 
@@ -339,13 +364,12 @@ def tile_hydraattention_pa_kernel(tc, x, mask, W_kv_words, W_kv_scales, b_kv, ou
 
         terms = []
         for t in range(TILES - LATE_TILES, TILES):
-            for strip in range(ACC_STRIPS, STRIPS):
+            for strip in product_order(t):
                 products = prod_of[t][:, strip * P : (strip + 1) * P]
                 terms.append((late_weights[:, t - (TILES - LATE_TILES), window(strip, 0)], products))
-        for strip in range(ACC_STRIPS):
+        for strip in range(ACC_FIRST, STRIPS):
             for s in range(SUMS):
-                running = acc_of[IMAGES - 1][:, s, strip * P : (strip + 1) * P]
-                terms.append((one_hot[:, window(strip, s)], running))
+                terms.append((one_hot[:, window(strip, s)], running_sum(IMAGES - 1, strip, s)))
         terms.append((sums[:], ident[:]))
         for i, (stationary, moving) in enumerate(terms):
             nc.tensor.matmul(

@@ -28,6 +28,7 @@ QUADRANT = 32
 BANK = 512
 BANKS_PER_TILE = KV // BANK
 KEY_BANKS = CHANNELS // BANK
+KV_HALVES = 2
 TILES_PER_IMAGE = PIXELS // P
 TILES = IMAGES * TILES_PER_IMAGE
 CHUNK_TILES = 2
@@ -60,7 +61,7 @@ def tile_hydraattention_pa_kernel(tc, x, mask, W_kv_words, W_kv_scales, b_kv, ou
         stage = ctx.enter_context(tc.tile_pool(name="stage", bufs=3))
         biased_pool = ctx.enter_context(tc.tile_pool(name="biased", bufs=6))
         scratch = ctx.enter_context(tc.tile_pool(name="scratch", bufs=2))
-        prod_pool = ctx.enter_context(tc.tile_pool(name="prod", bufs=4))
+        prod_pool = ctx.enter_context(tc.tile_pool(name="prod", bufs=5))
         acc_pool = ctx.enter_context(tc.tile_pool(name="acc", bufs=4))
         psum = ctx.enter_context(tc.psum_pool(name="psum", bufs=7))
         psum_sums = ctx.enter_context(tc.psum_pool(name="psum_sums", bufs=1))
@@ -69,7 +70,7 @@ def tile_hydraattention_pa_kernel(tc, x, mask, W_kv_words, W_kv_scales, b_kv, ou
         raw = keep.tile([P, CHUNKS, PASSES, PACK, CHUNK], BF16)
         x_codes = keep.tile([P, CHUNKS, PASSES * CHUNK], U32, align_bytes=64)
         x_scales = keep.tile([P, CHUNKS, PASSES * CHUNK], U8, align_bytes=64)
-        w_words = keep.tile([P, BANKS_PER_TILE, PASSES, 2 * BANK], U8, align_bytes=64)
+        w_words = keep.tile([P, KV_HALVES, PASSES, 2 * CHANNELS], U8, align_bytes=64)
         w_scales = keep.tile([P, PASSES, KV], U8, align_bytes=64)
         bias_rows = keep.tile([P, BANK], BF16)
         ident_bf16 = keep.tile([P, P], BF16)
@@ -117,10 +118,11 @@ def tile_hydraattention_pa_kernel(tc, x, mask, W_kv_words, W_kv_scales, b_kv, ou
                     in_=x_rows[b, g, :, :, quarter * CHUNK : (quarter + 1) * CHUNK],
                 )
 
-        def load_words(n):
+        def load_words(half):
+            columns = slice(2 * half * CHANNELS, 2 * (half + 1) * CHANNELS)
             nc.sync.dma_start(
-                out=w_words[:, n].bitcast(I32),
-                in_=W_kv_words.rearrange("g p byte -> p g byte")[:, :, 2 * n * BANK : 2 * (n + 1) * BANK].bitcast(I32),
+                out=w_words[:, half].bitcast(I32),
+                in_=W_kv_words.rearrange("g p byte -> p g byte")[:, :, columns].bitcast(I32),
             )
 
         load_chunk(0)
@@ -135,8 +137,6 @@ def tile_hydraattention_pa_kernel(tc, x, mask, W_kv_words, W_kv_scales, b_kv, ou
             out=mask_rows[0:TILES, :],
             in_=mask.rearrange("b o (i row) col -> (b o i) (row col)", i=TILES_PER_IMAGE),
         )
-        for n in range(KEY_BANKS, BANKS_PER_TILE):
-            load_words(n)
         load_chunk(1)
         for chunk in range(2, CHUNKS):
             load_chunk(chunk)
@@ -145,18 +145,27 @@ def tile_hydraattention_pa_kernel(tc, x, mask, W_kv_words, W_kv_scales, b_kv, ou
             grouped = stage.tile([P, PASSES, CHUNK, PACK], BF16, align_bytes=64)
             return grouped
 
-        def regroup(copy, chunk, grouped, g):
+        whole_chunk = slice(0, CHUNK)
+
+        def regroup(copy, chunk, grouped, g, pixels):
             copy(
-                out=grouped[:, g].rearrange("p (run e) j -> p run j e", e=RUN),
-                in_=raw[:, chunk, g].rearrange("p j (run e) -> p run j e", e=RUN),
+                out=grouped[:, g, pixels].rearrange("p (run e) j -> p run j e", e=RUN),
+                in_=raw[:, chunk, g, :, pixels].rearrange("p j (run e) -> p run j e", e=RUN),
             )
 
-        def quantise(chunk, grouped, first, last):
-            columns = slice(first * CHUNK, (last + 1) * CHUNK)
+        def quantise(chunk, grouped, g, pixels):
+            columns = slice(g * CHUNK + pixels.start, g * CHUNK + pixels.stop)
             nc.vector.quantize_mx(
                 out=x_codes[:, chunk, columns].bitcast(FP8X4),
                 scales=x_scales[:, chunk, columns],
-                in_=grouped[:, first : last + 1].rearrange("p g px j -> p (g px j)"),
+                in_=grouped[:, g, pixels].rearrange("p px j -> p (px j)"),
+            )
+
+        def quantise_chunk(chunk, grouped):
+            nc.vector.quantize_mx(
+                out=x_codes[:, chunk].bitcast(FP8X4),
+                scales=x_scales[:, chunk],
+                in_=grouped[:].rearrange("p g px j -> p (g px j)"),
             )
 
         def pool_strip(t, strip):
@@ -189,7 +198,15 @@ def tile_hydraattention_pa_kernel(tc, x, mask, W_kv_words, W_kv_scales, b_kv, ou
             for place in range(ACC_STRIPS):
                 job = waiting.pop(0) if waiting else None
                 jobs.append(lambda job=job: pool_running_sum(*job) if job else None)
-            return jobs + [lambda strip=strip: pool_strip(pool_tile, strip) for strip in product_order(pool_tile)]
+            pairs = []
+            half = ACC_FIRST // 2
+            if pool_tile >= 1:
+                pairs += [(pool_tile - 1, strip) for strip in product_order(pool_tile - 1)[half:]]
+            pairs += [(pool_tile, strip) for strip in product_order(pool_tile)[:half]]
+            if is_late(pool_tile + 1):
+                pairs += [(pool_tile, strip) for strip in product_order(pool_tile)[half:]]
+                jobs = []
+            return jobs + [lambda pair=pair: pool_strip(*pair) for pair in pairs]
 
         def accumulate(t):
             b, i = divmod(t, TILES_PER_IMAGE)
@@ -210,6 +227,7 @@ def tile_hydraattention_pa_kernel(tc, x, mask, W_kv_words, W_kv_scales, b_kv, ou
 
         def project_bank(t, n, jobs):
             chunk, place = divmod(t, CHUNK_TILES)
+            half, h = divmod(n, KEY_BANKS)
             acc = psum.tile([P, BANK], F32, tag="acc")
             for g in range(PASSES):
                 pixels = slice(g * CHUNK + place * P, g * CHUNK + (place + 1) * P)
@@ -217,7 +235,7 @@ def tile_hydraattention_pa_kernel(tc, x, mask, W_kv_words, W_kv_scales, b_kv, ou
                     out=acc[:],
                     lhsT=x_codes[:, chunk, pixels].bitcast(FP8X4),
                     lhsT_scale=x_scales[:, chunk, pixels],
-                    rhs=w_words[:, n, g].bitcast(FP4X4),
+                    rhs=w_words[:, half, g, 2 * h * BANK : 2 * (h + 1) * BANK].bitcast(FP4X4),
                     rhs_scale=w_scales[:, g, n * BANK : (n + 1) * BANK],
                     start=(g == 0),
                     stop=(g == PASSES - 1),
@@ -288,10 +306,16 @@ def tile_hydraattention_pa_kernel(tc, x, mask, W_kv_words, W_kv_scales, b_kv, ou
             nc.scalar.copy(out=bias[:, n * BANK : (n + 1) * BANK], in_=spread[:])
 
         first_grouped = new_grouped()
-        for g in range(PASSES):
-            regroup(nc.vector.tensor_copy, 0, first_grouped, g)
-        for g in range(PASSES):
-            quantise(0, first_grouped, g, g)
+        tile_pixels = [slice(0, P), slice(P, CHUNK)]
+        last_pass = PASSES - 1
+        for g in range(last_pass):
+            regroup(nc.vector.tensor_copy, 0, first_grouped, g, whole_chunk)
+        regroup(nc.vector.tensor_copy, 0, first_grouped, last_pass, tile_pixels[0])
+        regroup(nc.scalar.copy, 0, first_grouped, last_pass, tile_pixels[1])
+        for g in range(last_pass):
+            quantise(0, first_grouped, g, whole_chunk)
+        for pixels in tile_pixels:
+            quantise(0, first_grouped, last_pass, pixels)
         idle = psum.tile([P, BANK], F32, tag="acc")
         for n in range(WARM_UP):
             nc.tensor.matmul(out=idle[:], lhsT=warm[:, 0:P], rhs=warm[:], start=True, stop=True)
@@ -305,7 +329,7 @@ def tile_hydraattention_pa_kernel(tc, x, mask, W_kv_words, W_kv_scales, b_kv, ou
         nc.scalar.activation(out=mask_pair[:, :, 0], in_=mask_cols[:, 0:TILES], func=ACT.Copy, scale=-1.0, bias=1.0)
         nc.scalar.copy(out=mask_pair[:, :, 1], in_=mask_cols[:, 0:TILES])
         grouped_of = {1: new_grouped()}
-        regroup(nc.scalar.copy, 1, grouped_of[1], 0)
+        regroup(nc.scalar.copy, 1, grouped_of[1], 0, whole_chunk)
 
         for t in range(TILES):
             keys_of[t] = new_biased()
@@ -319,7 +343,7 @@ def tile_hydraattention_pa_kernel(tc, x, mask, W_kv_words, W_kv_scales, b_kv, ou
                 accumulate(t - 2)
             if t > 0 and opens_chunk(t + QUANTISE_AHEAD):
                 chunk = (t + QUANTISE_AHEAD) // CHUNK_TILES
-                quantise(chunk, grouped_of[chunk], 0, PASSES - 1)
+                quantise_chunk(chunk, grouped_of[chunk])
             new_product(t)
             if t == TILES - 1:
                 multiply(nc.vector, t, 0, middle)
@@ -331,15 +355,17 @@ def tile_hydraattention_pa_kernel(tc, x, mask, W_kv_words, W_kv_scales, b_kv, ou
                 multiply(nc.gpsimd, t, middle, CHANNELS)
                 multiply(nc.gpsimd, t, 0, middle)
             if t == 0:
-                regroup(nc.vector.tensor_copy, 1, grouped_of[1], 1)
-                quantise(1, grouped_of[1], 0, PASSES - 1)
+                regroup(nc.vector.tensor_copy, 1, grouped_of[1], 1, whole_chunk)
+                quantise_chunk(1, grouped_of[1])
             if t + 1 < TILES:
                 banks = [project_bank(t + 1, n, jobs) for n in range(BANKS_PER_TILE)]
+                for job in jobs:
+                    job()
             if opens_chunk(t + REGROUP_AHEAD):
                 chunk = (t + REGROUP_AHEAD) // CHUNK_TILES
                 grouped_of[chunk] = new_grouped()
                 for g in range(PASSES):
-                    regroup(nc.scalar.copy, chunk, grouped_of[chunk], g)
+                    regroup(nc.scalar.copy, chunk, grouped_of[chunk], g, whole_chunk)
 
         accumulate(TILES - 2)
         accumulate(TILES - 1)

from contextlib import ExitStack

import concourse.mybir as mybir
from concourse.masks import make_identity

F32 = mybir.dt.float32
BF16 = mybir.dt.bfloat16
U8 = mybir.dt.uint8
U32 = mybir.dt.uint32
I32 = mybir.dt.int32
FP8X4 = mybir.dt.float8_e4m3fn_x4
FP4X4 = mybir.dt.float4_e2m1fn_x4
ADD = mybir.AluOpType.add
MULT = mybir.AluOpType.mult
ACT = mybir.ActivationFunctionType

IMAGES = 2
CHANNELS = 1024
PIXELS = 1024
KV = 2 * CHANNELS

P = 128
PACK = 4
K_PASS = P * PACK
PASSES = CHANNELS // K_PASS
SCALE_ROWS = K_PASS // 32
QUADRANT = 32
BANK = 512
BANKS_PER_TILE = KV // BANK
KEY_BANKS = CHANNELS // BANK
KV_HALVES = 2
TILES_PER_IMAGE = PIXELS // P
TILES = IMAGES * TILES_PER_IMAGE
CHUNK_TILES = 2
CHUNK = CHUNK_TILES * P
CHUNKS = TILES // CHUNK_TILES
CHUNKS_PER_IMAGE = PIXELS // CHUNK
RUN = 4
STRIPS = CHANNELS // P
SUMS = 2
ROWS = SUMS * IMAGES * STRIPS
ACC_STRIPS = 2
ACC_WIDTH = ACC_STRIPS * P
ACC_FIRST = STRIPS - ACC_STRIPS
ACC_START = ACC_FIRST * P
LATE_TILES = 2
LATE_BASE = P
WARM_UP = 6
REGROUP_AHEAD = 4
QUANTISE_AHEAD = 2

assert STRIPS == BANKS_PER_TILE * PASSES

FLOPS = 2 * IMAGES * PIXELS * CHANNELS * KV


def tile_hydraattention_pa_kernel(tc, x, mask, W_kv_words, W_kv_scales, b_kv, out_0, out_1):
    nc = tc.nc
    with ExitStack() as ctx:
        keep = ctx.enter_context(tc.tile_pool(name="keep", bufs=1))
        stage = ctx.enter_context(tc.tile_pool(name="stage", bufs=3))
        biased_pool = ctx.enter_context(tc.tile_pool(name="biased", bufs=6))
        scratch = ctx.enter_context(tc.tile_pool(name="scratch", bufs=2))
        prod_pool = ctx.enter_context(tc.tile_pool(name="prod", bufs=5))
        acc_pool = ctx.enter_context(tc.tile_pool(name="acc", bufs=4))
        psum = ctx.enter_context(tc.psum_pool(name="psum", bufs=7))
        psum_sums = ctx.enter_context(tc.psum_pool(name="psum_sums", bufs=1))
        ctx.enter_context(tc.manual_schedule())

        raw = keep.tile([P, CHUNKS, PASSES, PACK, CHUNK], BF16)
        x_codes = keep.tile([P, CHUNKS, PASSES * CHUNK], U32, align_bytes=64)
        x_scales = keep.tile([P, CHUNKS, PASSES * CHUNK], U8, align_bytes=64)
        w_words = keep.tile([P, KV_HALVES, PASSES, 2 * CHANNELS], U8, align_bytes=64)
        w_scales = keep.tile([P, PASSES, KV], U8, align_bytes=64)
        bias_rows = keep.tile([P, BANK], BF16)
        ident_bf16 = keep.tile([P, P], BF16)
        warm = keep.tile([P, BANK], BF16)
        bias = keep.tile([P, KV], BF16)
        ident = keep.tile([P, P], F32)
        mask_rows = keep.tile([P, P], BF16)
        mask_pair = keep.tile([P, TILES, SUMS], F32)
        sumsq = keep.tile([P, TILES], F32)
        inv_norm = keep.tile([P, TILES], F32)
        weights = keep.tile([P, TILES, SUMS], F32)
        sums = keep.tile([P, P], F32)
        rows = keep.tile([P, P], F32)
        zeros = keep.tile([P, SUMS, ACC_WIDTH], F32)
        one_col = keep.tile([P, 1], F32)
        table_in = keep.tile([P, 1], F32)
        table_out = keep.tile([P, 1], F32)
        pooled = psum_sums.tile([P, TILES, STRIPS, SUMS], F32)
        late_weights = keep.tile([P, LATE_TILES, 2 * P], F32)
        one_hot = keep.tile([P, 2 * P], F32)

        nc.vector.memset(bias_rows[:].bitcast(I32), 0)
        nc.scalar.dma_start(out=bias_rows[0:BANKS_PER_TILE, :], in_=b_kv.rearrange("(n c) -> n c", c=BANK))
        nc.vector.memset(warm[:].bitcast(I32), 0)
        nc.vector.memset(mask_rows[:].bitcast(I32), 0)
        make_identity(nc, ident_bf16[:])
        nc.vector.memset(table_in[:], 1.0)
        nc.vector.memset(w_scales[:].rearrange("p g kv -> p (g kv)").bitcast(I32), 0)
        nc.scalar.activation(out=table_out[:], in_=table_in[:], func=ACT.Abs_reciprocal_sqrt)
        nc.gpsimd.memset(sums[:], 0.0)
        nc.gpsimd.memset(late_weights[:], 0.0)
        nc.gpsimd.memset(one_hot[:], 0.0)
        nc.gpsimd.memset(one_hot[:, LATE_BASE : LATE_BASE + 1], 1.0)
        nc.gpsimd.memset(zeros[:], 0.0)
        nc.gpsimd.memset(one_col[:], 1.0)
        make_identity(nc, ident[:])

        x_rows = x.rearrange("b (g p j) row col -> b g p j (row col)", g=PASSES, p=P, j=PACK)

        def load_chunk(chunk):
            b, quarter = divmod(chunk, CHUNKS_PER_IMAGE)
            for g in range(PASSES):
                nc.sync.dma_start(
                    out=raw[:, chunk, g],
                    in_=x_rows[b, g, :, :, quarter * CHUNK : (quarter + 1) * CHUNK],
                )

        def load_words(half):
            columns = slice(2 * half * CHANNELS, 2 * (half + 1) * CHANNELS)
            nc.sync.dma_start(
                out=w_words[:, half].bitcast(I32),
                in_=W_kv_words.rearrange("g p byte -> p g byte")[:, :, columns].bitcast(I32),
            )

        load_chunk(0)
        load_words(0)
        for r in range(PACK):
            nc.sync.dma_start(
                out=w_scales[r:P:QUADRANT, :, :].bitcast(I32),
                in_=W_kv_scales[:, r:SCALE_ROWS:PACK, :].rearrange("g q kv -> q g kv").bitcast(I32),
            )
        load_words(1)
        nc.sync.dma_start(
            out=mask_rows[0:TILES, :],
            in_=mask.rearrange("b o (i row) col -> (b o i) (row col)", i=TILES_PER_IMAGE),
        )
        load_chunk(1)
        for chunk in range(2, CHUNKS):
            load_chunk(chunk)

        def new_grouped():
            grouped = stage.tile([P, PASSES, CHUNK, PACK], BF16, align_bytes=64)
            return grouped

        whole_chunk = slice(0, CHUNK)

        def regroup(copy, chunk, grouped, g, pixels):
            copy(
                out=grouped[:, g, pixels].rearrange("p (run e) j -> p run j e", e=RUN),
                in_=raw[:, chunk, g, :, pixels].rearrange("p j (run e) -> p run j e", e=RUN),
            )

        def quantise(chunk, grouped, g, pixels):
            columns = slice(g * CHUNK + pixels.start, g * CHUNK + pixels.stop)
            nc.vector.quantize_mx(
                out=x_codes[:, chunk, columns].bitcast(FP8X4),
                scales=x_scales[:, chunk, columns],
                in_=grouped[:, g, pixels].rearrange("p px j -> p (px j)"),
            )

        def quantise_chunk(chunk, grouped):
            nc.vector.quantize_mx(
                out=x_codes[:, chunk].bitcast(FP8X4),
                scales=x_scales[:, chunk],
                in_=grouped[:].rearrange("p g px j -> p (g px j)"),
            )

        def pool_strip(t, strip):
            nc.tensor.matmul(
                out=pooled[:, t, strip, :],
                lhsT=prod_of[t][:, strip * P : (strip + 1) * P],
                rhs=weight_pair(t),
                start=True,
                stop=True,
            )

        def is_late(t):
            return t >= TILES - LATE_TILES

        def running_sum(b, strip, s):
            first = (strip - ACC_FIRST) * P
            return acc_of[b][:, s, first : first + P]

        def pool_running_sum(b, strip, s):
            nc.tensor.matmul(
                out=pooled[:, b * TILES_PER_IMAGE, strip, s : s + 1],
                lhsT=running_sum(b, strip, s),
                rhs=one_col[:],
                start=True,
                stop=True,
            )

        def jobs_behind_passes(pool_tile):
            jobs = []
            for place in range(ACC_STRIPS):
                job = waiting.pop(0) if waiting else None
                jobs.append(lambda job=job: pool_running_sum(*job) if job else None)
            pairs = []
            half = ACC_FIRST // 2
            if pool_tile >= 1:
                pairs += [(pool_tile - 1, strip) for strip in product_order(pool_tile - 1)[half:]]
            pairs += [(pool_tile, strip) for strip in product_order(pool_tile)[:half]]
            if is_late(pool_tile + 1):
                pairs += [(pool_tile, strip) for strip in product_order(pool_tile)[half:]]
                jobs = []
            return jobs + [lambda pair=pair: pool_strip(*pair) for pair in pairs]

        def accumulate(t):
            b, i = divmod(t, TILES_PER_IMAGE)
            before = zeros if i == 0 else acc_of[b]
            acc = acc_pool.tile([P, SUMS, ACC_WIDTH], F32)
            for s in range(SUMS):
                nc.vector.scalar_tensor_tensor(
                    out=acc[:, s, :],
                    in0=prod_of[t][:, ACC_START:CHANNELS],
                    scalar=weight_pair(t)[:, s : s + 1],
                    in1=before[:, s, :],
                    op0=MULT,
                    op1=ADD,
                )
            acc_of[b] = acc
            if t == TILES_PER_IMAGE - 1:
                waiting.extend((b, strip, s) for strip in range(ACC_FIRST, STRIPS) for s in range(SUMS))

        def project_bank(t, n, jobs):
            chunk, place = divmod(t, CHUNK_TILES)
            half, h = divmod(n, KEY_BANKS)
            acc = psum.tile([P, BANK], F32, tag="acc")
            for g in range(PASSES):
                pixels = slice(g * CHUNK + place * P, g * CHUNK + (place + 1) * P)
                nc.tensor.matmul_mx(
                    out=acc[:],
                    lhsT=x_codes[:, chunk, pixels].bitcast(FP8X4),
                    lhsT_scale=x_scales[:, chunk, pixels],
                    rhs=w_words[:, half, g, 2 * h * BANK : 2 * (h + 1) * BANK].bitcast(FP4X4),
                    rhs_scale=w_scales[:, g, n * BANK : (n + 1) * BANK],
                    start=(g == 0),
                    stop=(g == PASSES - 1),
                )
                if jobs:
                    jobs.pop(0)()
            return acc

        def new_biased():
            biased = biased_pool.tile([P, CHANNELS], F32)
            return biased

        def add_bias(biased, banks, n):
            h = n % KEY_BANKS
            nc.vector.tensor_tensor(
                out=biased[:, h * BANK : (h + 1) * BANK],
                in0=banks[n][:],
                in1=bias[:, n * BANK : (n + 1) * BANK],
                op=ADD,
            )

        def weight_pair(t):
            if is_late(t):
                return late_weights[:, t - (TILES - LATE_TILES), LATE_BASE : LATE_BASE + SUMS]
            return weights[:, t, :]

        def weigh(t):
            squares = scratch.tile([P, CHANNELS], F32)
            nc.scalar.activation(out=squares[:], in_=keys_of[t][:], func=ACT.Square, accum_out=sumsq[:, t : t + 1])
            nc.scalar.activation(out=inv_norm[:, t : t + 1], in_=sumsq[:, t : t + 1], func=ACT.Abs_reciprocal_sqrt)
            nc.scalar.activation(out=weight_pair(t), in_=mask_pair[:, t, :], func=ACT.Copy, scale=inv_norm[:, t : t + 1])

        middle = ACC_START // 2

        def product_order(t):
            strips = list(range(ACC_FIRST))
            half = middle // P
            return strips if t == TILES - 1 else strips[half:] + strips[:half]

        def new_product(t):
            prod = prod_pool.tile([P, CHANNELS], F32)
            prod_of[t] = prod

        def multiply(engine, t, first, last):
            part = slice(first, last)
            engine.tensor_tensor(
                out=prod_of[t][:, part], in0=keys_of[t][:, part], in1=values_of[t][:, part], op=MULT
            )

        def opens_chunk(t):
            return t < TILES and t % CHUNK_TILES == 0

        keys_of = {}
        values_of = {}
        prod_of = {}
        acc_of = {}
        waiting = []

        def spread_bias(n):
            spread = psum.tile([P, BANK], F32, tag="acc")
            nc.tensor.matmul(
                out=spread[:],
                lhsT=ident_bf16[:, n : n + 1].to_broadcast([P, P]),
                rhs=bias_rows[:],
                start=True,
                stop=True,
            )
            nc.scalar.copy(out=bias[:, n * BANK : (n + 1) * BANK], in_=spread[:])

        first_grouped = new_grouped()
        tile_pixels = [slice(0, P), slice(P, CHUNK)]
        last_pass = PASSES - 1
        for g in range(last_pass):
            regroup(nc.vector.tensor_copy, 0, first_grouped, g, whole_chunk)
        regroup(nc.vector.tensor_copy, 0, first_grouped, last_pass, tile_pixels[0])
        regroup(nc.scalar.copy, 0, first_grouped, last_pass, tile_pixels[1])
        for g in range(last_pass):
            quantise(0, first_grouped, g, whole_chunk)
        for pixels in tile_pixels:
            quantise(0, first_grouped, last_pass, pixels)
        idle = psum.tile([P, BANK], F32, tag="acc")
        for n in range(WARM_UP):
            nc.tensor.matmul(out=idle[:], lhsT=warm[:, 0:P], rhs=warm[:], start=True, stop=True)
        for n in range(BANKS_PER_TILE - 1):
            spread_bias(n)
        banks = [project_bank(0, 0, [])]
        spread_bias(BANKS_PER_TILE - 1)
        banks += [project_bank(0, n, []) for n in range(1, BANKS_PER_TILE)]
        mask_cols = psum.tile([P, P], BF16, tag="acc")
        nc.tensor.transpose(out=mask_cols[:], in_=mask_rows[:], identity=ident_bf16[:])
        nc.scalar.activation(out=mask_pair[:, :, 0], in_=mask_cols[:, 0:TILES], func=ACT.Copy, scale=-1.0, bias=1.0)
        nc.scalar.copy(out=mask_pair[:, :, 1], in_=mask_cols[:, 0:TILES])
        grouped_of = {1: new_grouped()}
        regroup(nc.scalar.copy, 1, grouped_of[1], 0, whole_chunk)

        for t in range(TILES):
            keys_of[t] = new_biased()
            for n in range(KEY_BANKS):
                add_bias(keys_of[t], banks, n)
            weigh(t)
            values_of[t] = new_biased()
            add_bias(values_of[t], banks, KEY_BANKS)
            jobs = jobs_behind_passes(t - 1) if t >= 1 else []
            if t >= 2:
                accumulate(t - 2)
            if t > 0 and opens_chunk(t + QUANTISE_AHEAD):
                chunk = (t + QUANTISE_AHEAD) // CHUNK_TILES
                quantise_chunk(chunk, grouped_of[chunk])
            new_product(t)
            if t == TILES - 1:
                multiply(nc.vector, t, 0, middle)
            add_bias(values_of[t], banks, KEY_BANKS + 1)
            if t == TILES - 1:
                multiply(nc.gpsimd, t, ACC_START, CHANNELS)
                multiply(nc.vector, t, middle, ACC_START)
            else:
                multiply(nc.gpsimd, t, middle, CHANNELS)
                multiply(nc.gpsimd, t, 0, middle)
            if t == 0:
                regroup(nc.vector.tensor_copy, 1, grouped_of[1], 1, whole_chunk)
                quantise_chunk(1, grouped_of[1])
            if t + 1 < TILES:
                banks = [project_bank(t + 1, n, jobs) for n in range(BANKS_PER_TILE)]
                for job in jobs:
                    job()
            if opens_chunk(t + REGROUP_AHEAD):
                chunk = (t + REGROUP_AHEAD) // CHUNK_TILES
                grouped_of[chunk] = new_grouped()
                for g in range(PASSES):
                    regroup(nc.scalar.copy, chunk, grouped_of[chunk], g, whole_chunk)

        accumulate(TILES - 2)
        accumulate(TILES - 1)

        sums_view = sums[:, 0:ROWS].rearrange("p (b strip s) -> p b strip s", b=IMAGES, s=SUMS)
        for b in range(IMAGES):
            first = b * TILES_PER_IMAGE
            end = min(first + TILES_PER_IMAGE, TILES - LATE_TILES)
            nc.vector.tensor_reduce(
                out=sums_view[:, b, 0:ACC_FIRST, :].rearrange("p strip s -> p (strip s)"),
                in_=pooled[:, first:end, 0:ACC_FIRST, :].rearrange("p i strip s -> p (strip s) i"),
                axis=mybir.AxisListType.X,
                op=ADD,
            )
        nc.vector.tensor_copy(out=sums_view[:, 0, ACC_FIRST:STRIPS, :], in_=pooled[:, 0, ACC_FIRST:STRIPS, :])

        turned = psum.tile([P, BANK], F32, tag="acc")

        def window(strip, s):
            start = LATE_BASE - (SUMS * (STRIPS * (IMAGES - 1) + strip) + s)
            return slice(start, start + P)

        terms = []
        for t in range(TILES - LATE_TILES, TILES):
            for strip in product_order(t):
                products = prod_of[t][:, strip * P : (strip + 1) * P]
                terms.append((late_weights[:, t - (TILES - LATE_TILES), window(strip, 0)], products))
        for strip in range(ACC_FIRST, STRIPS):
            for s in range(SUMS):
                terms.append((one_hot[:, window(strip, s)], running_sum(IMAGES - 1, strip, s)))
        terms.append((sums[:], ident[:]))
        for i, (stationary, moving) in enumerate(terms):
            nc.tensor.matmul(
                out=turned[:, 0:P], lhsT=stationary, rhs=moving, start=(i == 0), stop=(i == len(terms) - 1)
            )
        nc.vector.tensor_copy(out=rows[:], in_=turned[:, 0:P])
        for s, (queue, out) in enumerate(((nc.sync, out_0), (nc.scalar, out_1))):
            queue.dma_start(out=out.rearrange("b o (strip ch) -> (b o strip) ch", ch=P), in_=rows[s:ROWS:SUMS, :])
